import numpy as np
import ml_dtypes


def mxq(x, axis, fmt="e4m3"):
    dtype, down = {"e4m3": (ml_dtypes.float8_e4m3fn, 7), "e5m2": (ml_dtypes.float8_e5m2, 14)}[fmt]
    v = np.moveaxis(np.asarray(x, np.float32).astype(ml_dtypes.bfloat16).astype(np.float64), axis, -1)
    blocks = v.reshape(v.shape[:-1] + (-1, 32))
    amax = np.abs(blocks).max(-1, keepdims=True)
    byte = np.maximum(np.where(amax > 0, np.frexp(amax)[1] - 1 + 127, 0) - down, 1)
    scale = np.exp2(byte - 127.0)
    codes = (blocks / scale).astype(np.float32).astype(dtype).astype(np.float64)
    return np.moveaxis((codes * scale).reshape(v.shape), -1, axis)


WIDE = False


def mx_kscale(k):
    if not WIDE:
        return np.ones(k)
    levels = np.array([10, -10, 5, -5, 0])
    a = np.random.permutation(np.resize(levels, k // 512 * 4)).reshape(k // 512, 4)
    idx = np.arange(k)
    return np.exp2(a[idx // 512, idx % 128 // 32])


BF16 = ml_dtypes.bfloat16


def bf(x):
    return np.asarray(x, np.float32).astype(BF16)


def f64(x):
    return np.asarray(x).astype(np.float64)


B, DIM, HID, LS = 4096, 128, 512, 3
DL = DIM * LS
O1 = DL
O2 = O1 + DL
O3 = O2 + DL
O4 = O3 + DIM
O5 = O4 + DIM
P = O5 + DIM


def elu(v):
    return np.where(v > 0.0, v, np.exp(np.minimum(v, 0.0)) - 1.0)


def sigmoid(v):
    return 1.0 / (1.0 + np.exp(-v))


def col_scale():
    return np.concatenate([np.full(DL, 0.5), np.full(DL, 1.0), np.full(DL, 2.5 / np.sqrt(LS)),
                           np.full(DIM, 0.5), np.full(DIM, 8.0), np.full(DIM, 2.5)])


def setup_inputs():
    t = mx_kscale(HID)
    cs = col_scale()
    return {"x": bf(np.random.standard_normal((B, DIM))),
            "cond": bf(np.random.standard_normal((B, DIM))),
            "W1": bf(np.random.standard_normal((DIM, HID)) / np.sqrt(DIM) * t),
            "b1": bf(np.random.standard_normal(HID) * 0.5 * t),
            "W2": bf(np.random.standard_normal((HID, P)) * 1.2 / np.sqrt(HID) * cs / t[:, None]),
            "b2": bf(np.random.standard_normal(P) * 0.5 * cs)}


def reference(x, cond, W1, b1, W2, b2):
    x = f64(x)
    h = np.maximum(f64(cond) @ f64(W1) + f64(b1), 0.0)
    p = (mxq(h, 1, "e4m3") @ mxq(f64(W2), 0, "e4m3")) + f64(b2)
    n = x.shape[0]
    mat1 = p[:, :O1].reshape(n, DIM, LS)
    bias1 = p[:, O1:O2].reshape(n, DIM, LS)
    mat2 = p[:, O2:O3].reshape(n, DIM, LS)
    bias2 = p[:, O3:O4]
    eps = p[:, O4:O5] / 10.0
    alpha = p[:, O5:] / 10.0
    z = x[:, :, None] * mat1 + bias1
    num = np.sum(elu(z) * mat2, axis=-1)
    den = np.sum(np.maximum(-mat1 * mat2, 0.0), axis=-1) + 1.0
    return np.exp(alpha) * (x + 0.8 * sigmoid(eps) * num / den) + bias2

@@ -1,0 +1,265 @@
+from contextlib import ExitStack
+
+import concourse.mybir as mybir
+from concourse.masks import make_identity
+
+F32 = mybir.dt.float32
+BF16 = mybir.dt.bfloat16
+U32 = mybir.dt.uint32
+U8 = mybir.dt.uint8
+FP8X4 = mybir.dt.float8_e4m3fn_x4
+ACT = mybir.ActivationFunctionType
+ALU = mybir.AluOpType
+
+P = 128
+PACK = 4
+BATCH = 4096
+DIM = 128
+HID = 512
+LS = 3
+PARAMS = 1536
+COLS = 512
+BLOCKS = COLS // P
+ROUNDS = BATCH // COLS
+ROWS_PER_PARTITION = BATCH // P
+CHUNKS = PARAMS // P
+MAT1 = 0
+BIAS1 = 1
+MAT2 = 2
+BIAS2 = 9
+EPS = 10
+ALPHA = 11
+
+FLOPS = 2 * BATCH * DIM * HID + 2 * BATCH * HID * PARAMS
+
+
+def tile_cn_pa_t_kernel(tc, x, cond, W1, b1, W2, b2, out):
+    nc = tc.nc
+    x_rows = x.rearrange("(p r) d -> p r d", r=ROWS_PER_PARTITION)
+    cond_rows = cond.rearrange("(p r) d -> p r d", r=ROWS_PER_PARTITION)
+    out_rows = out.rearrange("(p r) d -> p r d", r=ROWS_PER_PARTITION)
+
+    with ExitStack() as ctx:
+        consts = ctx.enter_context(tc.tile_pool(name="consts", bufs=1))
+        rows = ctx.enter_context(tc.tile_pool(name="rows", bufs=3))
+        hidden = ctx.enter_context(tc.tile_pool(name="hidden", bufs=2))
+        work = ctx.enter_context(tc.tile_pool(name="work", bufs=4))
+        last = ctx.enter_context(tc.tile_pool(name="last", bufs=2))
+        psum_t = ctx.enter_context(tc.psum_pool(name="psum_t", bufs=1))
+        psum_h = ctx.enter_context(tc.psum_pool(name="psum_h", bufs=2))
+        psum_p = ctx.enter_context(tc.psum_pool(name="psum_p", bufs=3))
+        psum_f = ctx.enter_context(tc.psum_pool(name="psum_f", bufs=2))
+
+        w1_sb = consts.tile([P, HID], BF16)
+        nc.sync.dma_start(out=w1_sb[:], in_=W1)
+        b1_bf = consts.tile([P, PACK], BF16)
+        nc.sync.dma_start(out=b1_bf[:], in_=b1.rearrange("(p j) -> p j", j=PACK))
+        b2_ls_bf = consts.tile([P, 3, LS], BF16)
+        b2_one_bf = consts.tile([P, 3], BF16)
+        with nc.allow_non_contiguous_dma(reason="a bias vector, one feature to a partition"):
+            nc.sync.dma_start(
+                out=b2_ls_bf[:], in_=b2[0 : 3 * LS * DIM].rearrange("(s d l) -> d s l", s=3, l=LS)
+            )
+            nc.sync.dma_start(
+                out=b2_one_bf[:], in_=b2[3 * LS * DIM : PARAMS].rearrange("(s d) -> d s", s=3)
+            )
+        w2_raw = consts.tile([P, PACK, PARAMS], BF16)
+        nc.sync.dma_start(out=w2_raw[:], in_=W2.rearrange("(p j) c -> p j c", j=PACK))
+
+        ident_bf = consts.tile([P, P], BF16)
+        make_identity(nc, ident_bf[:])
+        ident_f = consts.tile([P, P], F32)
+        make_identity(nc, ident_f[:])
+        minus_one = consts.tile([P, 1], F32)
+        nc.vector.memset(minus_one[:], -1.0)
+        plus_one = consts.tile([P, 1], F32)
+        nc.vector.memset(plus_one[:], 1.0)
+
+        w1_r = consts.tile([P, PACK, P], BF16)
+        nc.vector.tensor_copy(out=w1_r[:], in_=w1_sb[:].rearrange("d (p j) -> d j p", j=PACK))
+        b1_f = consts.tile([P, PACK], F32)
+        nc.vector.tensor_copy(out=b1_f[:], in_=b1_bf[:])
+        bias_ls = consts.tile([P, 3, LS], F32)
+        nc.vector.tensor_copy(out=bias_ls[:], in_=b2_ls_bf[:])
+        bias1_plus_one = consts.tile([P, LS], F32)
+        nc.vector.tensor_scalar_add(out=bias1_plus_one[:], in0=bias_ls[:, BIAS1, :], scalar1=1.0)
+        bias_one = consts.tile([P, 3], F32)
+        nc.vector.tensor_copy(out=bias_one[:], in_=b2_one_bf[:])
+        eps_bias = consts.tile([P, 1], F32)
+        nc.vector.tensor_scalar_mul(out=eps_bias[:], in0=bias_one[:, 1:2], scalar1=0.05)
+        alpha_bias = consts.tile([P, 1], F32)
+        nc.vector.tensor_scalar_mul(out=alpha_bias[:], in0=bias_one[:, 2:3], scalar1=0.1)
+
+        w2_grp = consts.tile([P, CHUNKS, P, PACK], BF16, align_bytes=64)
+        for s in range(3):
+            src = w2_raw[:, :, s * LS * DIM : (s + 1) * LS * DIM].rearrange("p j (d l) -> p l d j", l=LS)
+            dst = w2_grp[:, s * LS : (s + 1) * LS, :, :]
+            if s % 2 == 0:
+                nc.vector.tensor_copy(out=dst, in_=src)
+            else:
+                nc.scalar.copy(out=dst, in_=src)
+        nc.scalar.copy(
+            out=w2_grp[:, BIAS2:CHUNKS, :, :],
+            in_=w2_raw[:, :, 3 * LS * DIM : PARAMS].rearrange("p j (s d) -> p s d j", s=3),
+        )
+        w2_codes = consts.tile([P, CHUNKS, P], U32, align_bytes=64)
+        w2_scales = consts.tile([P, CHUNKS, P], U8, align_bytes=64)
+        for c in range(0, CHUNKS, 4):
+            nc.vector.quantize_mx(
+                out=w2_codes[:, c : c + 4, :].rearrange("p c d -> p (c d)").bitcast(FP8X4),
+                scales=w2_scales[:, c : c + 4, :].rearrange("p c d -> p (c d)"),
+                in_=w2_grp[:, c : c + 4, :, :].rearrange("p c d j -> p (c d j)"),
+            )
+
+        def params(chunk, h_codes, h_scales):
+            bank = psum_p.tile([P, COLS], F32, name="bank")
+            nc.tensor.matmul_mx(
+                out=bank[:],
+                lhsT=w2_codes[:, chunk, :].bitcast(FP8X4),
+                lhsT_scale=w2_scales[:, chunk, :],
+                rhs=h_codes[:].bitcast(FP8X4),
+                rhs_scale=h_scales[:],
+                start=True,
+                stop=True,
+            )
+            return bank
+
+        def transposed_sum(terms):
+            total = psum_f.tile([P, BLOCKS, P], F32, name="total")
+            for r in range(BLOCKS):
+                for i, term in enumerate(terms):
+                    nc.tensor.matmul(
+                        out=total[:, r, :],
+                        lhsT=term[:, r * P : (r + 1) * P],
+                        rhs=ident_f[:],
+                        is_transpose=True,
+                        start=(i == 0),
+                        stop=(i == len(terms) - 1),
+                    )
+            return total
+
+        for t in range(ROUNDS):
+            block_rows = slice(t * BLOCKS, (t + 1) * BLOCKS)
+            cond_t = rows.tile([P, BLOCKS, DIM], BF16)
+            nc.sync.dma_start(out=cond_t[:], in_=cond_rows[:, block_rows, :])
+            x_t = rows.tile([P, BLOCKS, DIM], BF16)
+            nc.sync.dma_start(out=x_t[:], in_=x_rows[:, block_rows, :])
+            turned_ps = psum_t.tile([P, 2, COLS], BF16)
+            for r in range(BLOCKS):
+                nc.tensor.transpose(turned_ps[:, 0, r * P : (r + 1) * P], cond_t[:, r, :], ident_bf[:])
+            for r in range(BLOCKS):
+                nc.tensor.transpose(turned_ps[:, 1, r * P : (r + 1) * P], x_t[:, r, :], ident_bf[:])
+            turned = hidden.tile([P, 2, COLS], BF16)
+            nc.scalar.copy(out=turned[:], in_=turned_ps[:])
+            cond_T = turned[:, 0, :]
+            x_T = turned[:, 1, :]
+
+            planes = hidden.tile([P, PACK, COLS], BF16)
+            for j in range(PACK):
+                h_ps = psum_h.tile([P, COLS], F32)
+                nc.tensor.matmul(out=h_ps[:], lhsT=w1_r[:, j, :], rhs=cond_T, start=True, stop=True)
+                nc.scalar.activation(
+                    out=planes[:, j, :], in_=h_ps[:], func=ACT.Relu, bias=b1_f[:, j : j + 1], scale=1.0
+                )
+            grouped = hidden.tile([P, COLS, PACK], BF16, align_bytes=64)
+            nc.vector.tensor_copy(
+                out=grouped[:].rearrange("p (c i) j -> p c j i", i=4),
+                in_=planes[:].rearrange("p j (c i) -> p c j i", i=4),
+            )
+            h_codes = hidden.tile([P, COLS], U32, align_bytes=64)
+            h_scales = hidden.tile([P, COLS], U8, align_bytes=64)
+            nc.vector.quantize_mx(
+                out=h_codes[:].bitcast(FP8X4),
+                scales=h_scales[:],
+                in_=grouped[:].rearrange("p w j -> p (w j)"),
+            )
+
+            num_terms = []
+            den_terms = []
+            for l in range(LS):
+                mat2_ps = params(MAT2 * LS + l, h_codes, h_scales)
+                mat2 = work.tile([P, COLS], F32)
+                nc.scalar.activation(
+                    out=mat2[:], in_=mat2_ps[:], func=ACT.Identity, bias=bias_ls[:, MAT2, l : l + 1], scale=1.0
+                )
+                mat1_ps = params(MAT1 * LS + l, h_codes, h_scales)
+                bias1_ps = params(BIAS1 * LS + l, h_codes, h_scales)
+                x_mat1 = work.tile([P, COLS], F32)
+                nc.vector.scalar_tensor_tensor(
+                    out=x_mat1[:], in0=mat1_ps[:], scalar=bias_ls[:, MAT1, l : l + 1], in1=x_T,
+                    op0=ALU.add, op1=ALU.mult,
+                )
+                z_plus_one = work.tile([P, COLS], F32)
+                nc.vector.scalar_tensor_tensor(
+                    out=z_plus_one[:], in0=bias1_ps[:], scalar=bias1_plus_one[:, l : l + 1], in1=x_mat1[:],
+                    op0=ALU.add, op1=ALU.add,
+                )
+                mat1_mat2 = work.tile([P, COLS], F32)
+                nc.vector.scalar_tensor_tensor(
+                    out=mat1_mat2[:], in0=mat1_ps[:], scalar=bias_ls[:, MAT1, l : l + 1], in1=mat2[:],
+                    op0=ALU.add, op1=ALU.mult,
+                )
+                exp_z = work.tile([P, COLS], F32)
+                nc.scalar.activation(
+                    out=exp_z[:], in_=z_plus_one[:], func=ACT.Exp, bias=minus_one[:], scale=1.0
+                )
+                den_term = work.tile([P, COLS], F32, bufs=2 * LS)
+                nc.scalar.activation(out=den_term[:], in_=mat1_mat2[:], func=ACT.Relu, scale=-1.0)
+                elu_plus_one = work.tile([P, COLS], F32)
+                nc.vector.scalar_tensor_tensor(
+                    out=elu_plus_one[:], in0=exp_z[:], scalar=1.0, in1=z_plus_one[:],
+                    op0=ALU.min, op1=ALU.max,
+                )
+                num_term = work.tile([P, COLS], F32, bufs=2 * LS)
+                nc.vector.scalar_tensor_tensor(
+                    out=num_term[:], in0=elu_plus_one[:], scalar=-1.0, in1=mat2[:],
+                    op0=ALU.add, op1=ALU.mult,
+                )
+                num_terms.append(num_term)
+                den_terms.append(den_term)
+
+            eps_ps = params(EPS, h_codes, h_scales)
+            tanh_eps = last.tile([P, COLS], F32)
+            nc.scalar.activation(out=tanh_eps[:], in_=eps_ps[:], func=ACT.Tanh, bias=eps_bias[:], scale=0.05)
+            alpha_ps = params(ALPHA, h_codes, h_scales)
+            exp_alpha = last.tile([P, COLS], F32)
+            nc.scalar.activation(out=exp_alpha[:], in_=alpha_ps[:], func=ACT.Exp, bias=alpha_bias[:], scale=0.1)
+            bias2_ps = params(BIAS2, h_codes, h_scales)
+            bias2 = last.tile([P, COLS], F32)
+            nc.scalar.activation(
+                out=bias2[:], in_=bias2_ps[:], func=ACT.Identity, bias=bias_one[:, 0:1], scale=1.0
+            )
+            gate = last.tile([P, COLS], F32)
+            nc.vector.scalar_tensor_tensor(
+                out=gate[:], in0=tanh_eps[:], scalar=1.0, in1=exp_alpha[:], op0=ALU.add, op1=ALU.mult
+            )
+            x_scaled = last.tile([P, COLS], F32)
+            nc.vector.tensor_tensor(out=x_scaled[:], in0=exp_alpha[:], in1=x_T, op=ALU.mult)
+
+            den_ps = transposed_sum(den_terms)
+            log_den = last.tile([P, COLS], F32)
+            nc.scalar.activation(
+                out=log_den[:], in_=den_ps[:].rearrange("p r d -> p (r d)"), func=ACT.Ln, bias=plus_one[:], scale=1.0
+            )
+            inv_den = last.tile([P, COLS], F32)
+            nc.scalar.activation(out=inv_den[:], in_=log_den[:], func=ACT.Exp, scale=-1.0)
+            num_ps = transposed_sum(num_terms)
+            ratio = last.tile([P, COLS], F32)
+            nc.vector.scalar_tensor_tensor(
+                out=ratio[:], in0=num_ps[:].rearrange("p r d -> p (r d)"), scalar=0.4, in1=inv_den[:],
+                op0=ALU.mult, op1=ALU.mult,
+            )
+            gate_ps = transposed_sum([gate])
+            moved = last.tile([P, COLS], F32)
+            nc.vector.tensor_tensor(
+                out=moved[:], in0=gate_ps[:].rearrange("p r d -> p (r d)"), in1=ratio[:], op=ALU.mult
+            )
+            base_ps = transposed_sum([x_scaled, bias2])
+            result = last.tile([P, BLOCKS, DIM], F32)
+            nc.vector.tensor_tensor(
+                out=result[:].rearrange("p r d -> p (r d)"),
+                in0=base_ps[:].rearrange("p r d -> p (r d)"),
+                in1=moved[:],
+                op=ALU.add,
+            )
+            nc.sync.dma_start(out=out_rows[:, block_rows, :], in_=result[:])

@@ -23,12 +23,15 @@ BLOCKS = COLS // P
 ROUNDS = BATCH // COLS
 ROWS_PER_PARTITION = BATCH // P
 CHUNKS = PARAMS // P
+SECTION = LS * DIM
 MAT1 = 0
 BIAS1 = 1
 MAT2 = 2
 BIAS2 = 9
 EPS = 10
 ALPHA = 11
+PSUM_BANKS = 8
+LOWEST = -3.0e38
 
 FLOPS = 2 * BATCH * DIM * HID + 2 * BATCH * HID * PARAMS
 
@@ -40,31 +43,47 @@ def tile_cn_pa_t_kernel(tc, x, cond, W1, b1, W2, b2, out):
     out_rows = out.rearrange("(p r) d -> p r d", r=ROWS_PER_PARTITION)
 
     with ExitStack() as ctx:
+        ctx.enter_context(tc.manual_schedule())
         consts = ctx.enter_context(tc.tile_pool(name="consts", bufs=1))
-        rows = ctx.enter_context(tc.tile_pool(name="rows", bufs=3))
+        rows = ctx.enter_context(tc.tile_pool(name="rows", bufs=ROUNDS))
         hidden = ctx.enter_context(tc.tile_pool(name="hidden", bufs=2))
-        work = ctx.enter_context(tc.tile_pool(name="work", bufs=4))
+        work = ctx.enter_context(tc.tile_pool(name="work", bufs=LS + 1))
+        kept = ctx.enter_context(tc.tile_pool(name="kept", bufs=3))
         last = ctx.enter_context(tc.tile_pool(name="last", bufs=2))
-        psum_t = ctx.enter_context(tc.psum_pool(name="psum_t", bufs=1))
-        psum_h = ctx.enter_context(tc.psum_pool(name="psum_h", bufs=2))
-        psum_p = ctx.enter_context(tc.psum_pool(name="psum_p", bufs=3))
-        psum_f = ctx.enter_context(tc.psum_pool(name="psum_f", bufs=2))
+        psum = ctx.enter_context(tc.psum_pool(name="psum", bufs=PSUM_BANKS))
+
+        def bank(shape, dtype):
+            return psum.tile(shape, dtype, name="bank", tag="bank")
+
+        cond_t = {}
+        x_t = {}
+
+        def load_rows(t):
+            block_rows = slice(t * BLOCKS, (t + 1) * BLOCKS)
+            cond_t[t] = rows.tile([P, BLOCKS, DIM], BF16, name="cond_t")
+            nc.sync.dma_start(out=cond_t[t][:], in_=cond_rows[:, block_rows, :])
+            x_t[t] = rows.tile([P, BLOCKS, DIM], BF16, name="x_t")
+            nc.sync.dma_start(out=x_t[t][:], in_=x_rows[:, block_rows, :])
 
         w1_sb = consts.tile([P, HID], BF16)
         nc.sync.dma_start(out=w1_sb[:], in_=W1)
-        b1_bf = consts.tile([P, PACK], BF16)
-        nc.sync.dma_start(out=b1_bf[:], in_=b1.rearrange("(p j) -> p j", j=PACK))
+        b1_row = consts.tile([P, HID], BF16)
+        nc.vector.memset(b1_row[:], 0.0)
+        nc.sync.dma_start(out=b1_row[0:1, :], in_=b1.rearrange("(o k) -> o k", o=1))
+        load_rows(0)
+        w2_rows = W2.rearrange("(p j) c -> p j c", j=PACK)
+        w2_raw = []
+        for s in range(4):
+            w2_part = consts.tile([P, PACK, SECTION], BF16, name="w2_raw%d" % s)
+            nc.sync.dma_start(out=w2_part[:], in_=w2_rows[:, :, s * SECTION : (s + 1) * SECTION])
+            w2_raw.append(w2_part)
         b2_ls_bf = consts.tile([P, 3, LS], BF16)
         b2_one_bf = consts.tile([P, 3], BF16)
         with nc.allow_non_contiguous_dma(reason="a bias vector, one feature to a partition"):
-            nc.sync.dma_start(
-                out=b2_ls_bf[:], in_=b2[0 : 3 * LS * DIM].rearrange("(s d l) -> d s l", s=3, l=LS)
-            )
-            nc.sync.dma_start(
-                out=b2_one_bf[:], in_=b2[3 * LS * DIM : PARAMS].rearrange("(s d) -> d s", s=3)
-            )
-        w2_raw = consts.tile([P, PACK, PARAMS], BF16)
-        nc.sync.dma_start(out=w2_raw[:], in_=W2.rearrange("(p j) c -> p j c", j=PACK))
+            nc.sync.dma_start(out=b2_ls_bf[:], in_=b2[0 : 3 * SECTION].rearrange("(s d l) -> d s l", s=3, l=LS))
+            nc.sync.dma_start(out=b2_one_bf[:], in_=b2[3 * SECTION : PARAMS].rearrange("(s d) -> d s", s=3))
+        for t in range(1, ROUNDS):
+            load_rows(t)
 
         ident_bf = consts.tile([P, P], BF16)
         make_identity(nc, ident_bf[:])
@@ -74,11 +93,76 @@ def tile_cn_pa_t_kernel(tc, x, cond, W1, b1, W2, b2, out):
         nc.vector.memset(minus_one[:], -1.0)
         plus_one = consts.tile([P, 1], F32)
         nc.vector.memset(plus_one[:], 1.0)
-
         w1_r = consts.tile([P, PACK, P], BF16)
         nc.vector.tensor_copy(out=w1_r[:], in_=w1_sb[:].rearrange("d (p j) -> d j p", j=PACK))
-        b1_f = consts.tile([P, PACK], F32)
-        nc.vector.tensor_copy(out=b1_f[:], in_=b1_bf[:])
+        ones = consts.tile([P, P], BF16)
+        nc.vector.memset(ones[:], 1.0)
+        b1_ps = bank([P, HID], F32)
+        nc.tensor.matmul(out=b1_ps[:], lhsT=ones[:], rhs=b1_row[:], start=True, stop=True)
+        b1_rows = consts.tile([P, PACK, P], F32)
+        nc.vector.tensor_copy(out=b1_rows[:], in_=b1_ps[:].rearrange("w (p j) -> w j p", j=PACK))
+
+        turned = {}
+        grouped = {}
+        h_codes = {}
+        h_scales = {}
+
+        def turn(t):
+            turned_ps = bank([P, 2, COLS], BF16)
+            for r in range(BLOCKS):
+                nc.tensor.transpose(turned_ps[:, 0, r * P : (r + 1) * P], cond_t[t][:, r, :], ident_bf[:])
+            for r in range(BLOCKS):
+                nc.tensor.transpose(turned_ps[:, 1, r * P : (r + 1) * P], x_t[t][:, r, :], ident_bf[:])
+            turned[t] = hidden.tile([P, 2, COLS], BF16, name="turned", bufs=3)
+            nc.scalar.copy(out=turned[t][:], in_=turned_ps[:])
+
+        def hidden_block(t, r):
+            if r == 0:
+                grouped[t] = hidden.tile([P, COLS, PACK], BF16, name="grouped", align_bytes=64)
+            h_ps = bank([P, PACK, P], F32)
+            for j in range(PACK):
+                nc.tensor.matmul(
+                    out=h_ps[:, j, :], lhsT=b1_rows[:, j, :], rhs=ident_f[:], is_transpose=True, start=True, stop=False
+                )
+                nc.tensor.matmul(
+                    out=h_ps[:, j, :], lhsT=w1_r[:, j, :], rhs=turned[t][:, 0, r * P : (r + 1) * P],
+                    start=False, stop=True,
+                )
+            nc.scalar.activation(
+                out=grouped[t][:, r * P : (r + 1) * P, :], in_=h_ps[:].rearrange("p j w -> p w j"), func=ACT.Relu
+            )
+
+        def quantise_hidden(t):
+            h_codes[t] = hidden.tile([P, COLS], U32, name="h_codes", align_bytes=64)
+            h_scales[t] = hidden.tile([P, COLS], U8, name="h_scales", align_bytes=64)
+            nc.vector.quantize_mx(
+                out=h_codes[t][:].bitcast(FP8X4),
+                scales=h_scales[t][:],
+                in_=grouped[t][:].rearrange("p w j -> p (w j)"),
+            )
+
+        turn(0)
+        for r in range(BLOCKS):
+            hidden_block(0, r)
+        turn(1)
+
+        w2_grp = consts.tile([P, CHUNKS, P, PACK], BF16, align_bytes=64)
+        for s in range(3):
+            nc.vector.tensor_copy(
+                out=w2_grp[:, s * LS : (s + 1) * LS, :, :], in_=w2_raw[s][:].rearrange("p j (d l) -> p l d j", l=LS)
+            )
+        quantise_hidden(0)
+        nc.vector.tensor_copy(
+            out=w2_grp[:, BIAS2:CHUNKS, :, :], in_=w2_raw[3][:].rearrange("p j (s d) -> p s d j", s=3)
+        )
+        w2_codes = consts.tile([P, CHUNKS, P], U32, align_bytes=64)
+        w2_scales = consts.tile([P, CHUNKS, P], U8, align_bytes=64)
+        for c in range(0, CHUNKS, 4):
+            nc.vector.quantize_mx(
+                out=w2_codes[:, c : c + 4, :].rearrange("p c d -> p (c d)").bitcast(FP8X4),
+                scales=w2_scales[:, c : c + 4, :].rearrange("p c d -> p (c d)"),
+                in_=w2_grp[:, c : c + 4, :, :].rearrange("p c d j -> p (c d j)"),
+            )
         bias_ls = consts.tile([P, 3, LS], F32)
         nc.vector.tensor_copy(out=bias_ls[:], in_=b2_ls_bf[:])
         bias1_plus_one = consts.tile([P, LS], F32)
@@ -90,42 +174,21 @@ def tile_cn_pa_t_kernel(tc, x, cond, W1, b1, W2, b2, out):
         alpha_bias = consts.tile([P, 1], F32)
         nc.vector.tensor_scalar_mul(out=alpha_bias[:], in0=bias_one[:, 2:3], scalar1=0.1)
 
-        w2_grp = consts.tile([P, CHUNKS, P, PACK], BF16, align_bytes=64)
-        for s in range(3):
-            src = w2_raw[:, :, s * LS * DIM : (s + 1) * LS * DIM].rearrange("p j (d l) -> p l d j", l=LS)
-            dst = w2_grp[:, s * LS : (s + 1) * LS, :, :]
-            if s % 2 == 0:
-                nc.vector.tensor_copy(out=dst, in_=src)
-            else:
-                nc.scalar.copy(out=dst, in_=src)
-        nc.scalar.copy(
-            out=w2_grp[:, BIAS2:CHUNKS, :, :],
-            in_=w2_raw[:, :, 3 * LS * DIM : PARAMS].rearrange("p j (s d) -> p s d j", s=3),
-        )
-        w2_codes = consts.tile([P, CHUNKS, P], U32, align_bytes=64)
-        w2_scales = consts.tile([P, CHUNKS, P], U8, align_bytes=64)
-        for c in range(0, CHUNKS, 4):
-            nc.vector.quantize_mx(
-                out=w2_codes[:, c : c + 4, :].rearrange("p c d -> p (c d)").bitcast(FP8X4),
-                scales=w2_scales[:, c : c + 4, :].rearrange("p c d -> p (c d)"),
-                in_=w2_grp[:, c : c + 4, :, :].rearrange("p c d j -> p (c d j)"),
-            )
-
-        def params(chunk, h_codes, h_scales):
-            bank = psum_p.tile([P, COLS], F32, name="bank")
+        def params(t, chunk):
+            p_ps = bank([P, COLS], F32)
             nc.tensor.matmul_mx(
-                out=bank[:],
+                out=p_ps[:],
                 lhsT=w2_codes[:, chunk, :].bitcast(FP8X4),
                 lhsT_scale=w2_scales[:, chunk, :],
-                rhs=h_codes[:].bitcast(FP8X4),
-                rhs_scale=h_scales[:],
+                rhs=h_codes[t][:].bitcast(FP8X4),
+                rhs_scale=h_scales[t][:],
                 start=True,
                 stop=True,
             )
-            return bank
+            return p_ps
 
         def transposed_sum(terms):
-            total = psum_f.tile([P, BLOCKS, P], F32, name="total")
+            total = bank([P, BLOCKS, P], F32)
             for r in range(BLOCKS):
                 for i, term in enumerate(terms):
                     nc.tensor.matmul(
@@ -136,130 +199,151 @@ def tile_cn_pa_t_kernel(tc, x, cond, W1, b1, W2, b2, out):
                         start=(i == 0),
                         stop=(i == len(terms) - 1),
                     )
-            return total
+            return total[:].rearrange("p r d -> p (r d)")
 
-        for t in range(ROUNDS):
-            block_rows = slice(t * BLOCKS, (t + 1) * BLOCKS)
-            cond_t = rows.tile([P, BLOCKS, DIM], BF16)
-            nc.sync.dma_start(out=cond_t[:], in_=cond_rows[:, block_rows, :])
-            x_t = rows.tile([P, BLOCKS, DIM], BF16)
-            nc.sync.dma_start(out=x_t[:], in_=x_rows[:, block_rows, :])
-            turned_ps = psum_t.tile([P, 2, COLS], BF16)
-            for r in range(BLOCKS):
-                nc.tensor.transpose(turned_ps[:, 0, r * P : (r + 1) * P], cond_t[:, r, :], ident_bf[:])
-            for r in range(BLOCKS):
-                nc.tensor.transpose(turned_ps[:, 1, r * P : (r + 1) * P], x_t[:, r, :], ident_bf[:])
-            turned = hidden.tile([P, 2, COLS], BF16)
-            nc.scalar.copy(out=turned[:], in_=turned_ps[:])
-            cond_T = turned[:, 0, :]
-            x_T = turned[:, 1, :]
+        mat2 = {}
+        z_plus_one = {}
+        mat1_mat2 = {}
+        x_mat1 = {}
+        tanh_eps = {}
+        exp_alpha = {}
+        bias2 = {}
+        exp_z = {}
+        num_terms = {}
+        den_terms = {}
+        gate_terms = {}
+        base_terms = {}
+        log_den = {}
+        inv_den = {}
 
-            planes = hidden.tile([P, PACK, COLS], BF16)
-            for j in range(PACK):
-                h_ps = psum_h.tile([P, COLS], F32)
-                nc.tensor.matmul(out=h_ps[:], lhsT=w1_r[:, j, :], rhs=cond_T, start=True, stop=True)
-                nc.scalar.activation(
-                    out=planes[:, j, :], in_=h_ps[:], func=ACT.Relu, bias=b1_f[:, j : j + 1], scale=1.0
-                )
-            grouped = hidden.tile([P, COLS, PACK], BF16, align_bytes=64)
-            nc.vector.tensor_copy(
-                out=grouped[:].rearrange("p (c i) j -> p c j i", i=4),
-                in_=planes[:].rearrange("p j (c i) -> p c j i", i=4),
-            )
-            h_codes = hidden.tile([P, COLS], U32, align_bytes=64)
-            h_scales = hidden.tile([P, COLS], U8, align_bytes=64)
-            nc.vector.quantize_mx(
-                out=h_codes[:].bitcast(FP8X4),
-                scales=h_scales[:],
-                in_=grouped[:].rearrange("p w j -> p (w j)"),
-            )
-
-            num_terms = []
-            den_terms = []
-            for l in range(LS):
-                mat2_ps = params(MAT2 * LS + l, h_codes, h_scales)
-                mat2 = work.tile([P, COLS], F32)
-                nc.scalar.activation(
-                    out=mat2[:], in_=mat2_ps[:], func=ACT.Identity, bias=bias_ls[:, MAT2, l : l + 1], scale=1.0
-                )
-                mat1_ps = params(MAT1 * LS + l, h_codes, h_scales)
-                bias1_ps = params(BIAS1 * LS + l, h_codes, h_scales)
-                x_mat1 = work.tile([P, COLS], F32)
-                nc.vector.scalar_tensor_tensor(
-                    out=x_mat1[:], in0=mat1_ps[:], scalar=bias_ls[:, MAT1, l : l + 1], in1=x_T,
-                    op0=ALU.add, op1=ALU.mult,
-                )
-                z_plus_one = work.tile([P, COLS], F32)
-                nc.vector.scalar_tensor_tensor(
-                    out=z_plus_one[:], in0=bias1_ps[:], scalar=bias1_plus_one[:, l : l + 1], in1=x_mat1[:],
-                    op0=ALU.add, op1=ALU.add,
-                )
-                mat1_mat2 = work.tile([P, COLS], F32)
-                nc.vector.scalar_tensor_tensor(
-                    out=mat1_mat2[:], in0=mat1_ps[:], scalar=bias_ls[:, MAT1, l : l + 1], in1=mat2[:],
-                    op0=ALU.add, op1=ALU.mult,
-                )
-                exp_z = work.tile([P, COLS], F32)
-                nc.scalar.activation(
-                    out=exp_z[:], in_=z_plus_one[:], func=ACT.Exp, bias=minus_one[:], scale=1.0
-                )
-                den_term = work.tile([P, COLS], F32, bufs=2 * LS)
-                nc.scalar.activation(out=den_term[:], in_=mat1_mat2[:], func=ACT.Relu, scale=-1.0)
-                elu_plus_one = work.tile([P, COLS], F32)
-                nc.vector.scalar_tensor_tensor(
-                    out=elu_plus_one[:], in0=exp_z[:], scalar=1.0, in1=z_plus_one[:],
-                    op0=ALU.min, op1=ALU.max,
-                )
-                num_term = work.tile([P, COLS], F32, bufs=2 * LS)
-                nc.vector.scalar_tensor_tensor(
-                    out=num_term[:], in0=elu_plus_one[:], scalar=-1.0, in1=mat2[:],
-                    op0=ALU.add, op1=ALU.mult,
-                )
-                num_terms.append(num_term)
-                den_terms.append(den_term)
-
-            eps_ps = params(EPS, h_codes, h_scales)
-            tanh_eps = last.tile([P, COLS], F32)
-            nc.scalar.activation(out=tanh_eps[:], in_=eps_ps[:], func=ACT.Tanh, bias=eps_bias[:], scale=0.05)
-            alpha_ps = params(ALPHA, h_codes, h_scales)
-            exp_alpha = last.tile([P, COLS], F32)
-            nc.scalar.activation(out=exp_alpha[:], in_=alpha_ps[:], func=ACT.Exp, bias=alpha_bias[:], scale=0.1)
-            bias2_ps = params(BIAS2, h_codes, h_scales)
-            bias2 = last.tile([P, COLS], F32)
+        def network_products(t, l):
+            mat2_ps = params(t, MAT2 * LS + l)
+            mat2[t, l] = work.tile([P, COLS], F32, name="mat2")
             nc.scalar.activation(
-                out=bias2[:], in_=bias2_ps[:], func=ACT.Identity, bias=bias_one[:, 0:1], scale=1.0
+                out=mat2[t, l][:], in_=mat2_ps[:], func=ACT.Identity, bias=bias_ls[:, MAT2, l : l + 1], scale=1.0
             )
-            gate = last.tile([P, COLS], F32)
+            mat1_ps = params(t, MAT1 * LS + l)
+            if l == 0:
+                mat1_mat2[t] = work.tile([P, LS, COLS], F32, name="mat1_mat2", bufs=2)
             nc.vector.scalar_tensor_tensor(
-                out=gate[:], in0=tanh_eps[:], scalar=1.0, in1=exp_alpha[:], op0=ALU.add, op1=ALU.mult
+                out=mat1_mat2[t][:, l, :], in0=mat1_ps[:], scalar=bias_ls[:, MAT1, l : l + 1], in1=mat2[t, l][:],
+                op0=ALU.add, op1=ALU.mult,
             )
-            x_scaled = last.tile([P, COLS], F32)
-            nc.vector.tensor_tensor(out=x_scaled[:], in0=exp_alpha[:], in1=x_T, op=ALU.mult)
+            x_mat1[t, l] = work.tile([P, COLS], F32, name="x_mat1")
+            nc.vector.scalar_tensor_tensor(
+                out=x_mat1[t, l][:], in0=mat1_ps[:], scalar=bias_ls[:, MAT1, l : l + 1], in1=turned[t][:, 1, :],
+                op0=ALU.add, op1=ALU.mult,
+            )
 
-            den_ps = transposed_sum(den_terms)
-            log_den = last.tile([P, COLS], F32)
-            nc.scalar.activation(
-                out=log_den[:], in_=den_ps[:].rearrange("p r d -> p (r d)"), func=ACT.Ln, bias=plus_one[:], scale=1.0
+        def denominator_terms(t):
+            den_terms[t] = kept.tile([P, LS, COLS], F32, name="den_terms")
+            nc.gpsimd.tensor_scalar(
+                out=den_terms[t][:], in0=mat1_mat2[t][:], scalar1=0.0, scalar2=LOWEST, op0=ALU.min, op1=ALU.max
             )
-            inv_den = last.tile([P, COLS], F32)
-            nc.scalar.activation(out=inv_den[:], in_=log_den[:], func=ACT.Exp, scale=-1.0)
-            num_ps = transposed_sum(num_terms)
+
+        def network_exp(t, l):
+            bias1_ps = params(t, BIAS1 * LS + l)
+            z_plus_one[t, l] = work.tile([P, COLS], F32, name="z_plus_one")
+            nc.vector.scalar_tensor_tensor(
+                out=z_plus_one[t, l][:], in0=bias1_ps[:], scalar=bias1_plus_one[:, l : l + 1], in1=x_mat1[t, l][:],
+                op0=ALU.add, op1=ALU.add,
+            )
+            exp_z[t, l] = work.tile([P, COLS], F32, name="exp_z")
+            nc.scalar.activation(
+                out=exp_z[t, l][:], in_=z_plus_one[t, l][:], func=ACT.Exp, bias=minus_one[:], scale=1.0
+            )
+
+        def network_terms(t, l):
+            elu_plus_one = work.tile([P, COLS], F32, bufs=2)
+            nc.vector.scalar_tensor_tensor(
+                out=elu_plus_one[:], in0=exp_z[t, l][:], scalar=1.0, in1=z_plus_one[t, l][:],
+                op0=ALU.min, op1=ALU.max,
+            )
+            num_term = kept.tile([P, COLS], F32, bufs=4 * LS)
+            nc.vector.scalar_tensor_tensor(
+                out=num_term[:], in0=elu_plus_one[:], scalar=-1.0, in1=mat2[t, l][:],
+                op0=ALU.add, op1=ALU.mult,
+            )
+            num_terms[t] = num_terms.get(t, []) + [num_term]
+
+        def gates(t):
+            eps_ps = params(t, EPS)
+            tanh_eps[t] = kept.tile([P, COLS], F32, name="tanh_eps")
+            nc.scalar.activation(out=tanh_eps[t][:], in_=eps_ps[:], func=ACT.Tanh, bias=eps_bias[:], scale=0.05)
+            alpha_ps = params(t, ALPHA)
+            exp_alpha[t] = kept.tile([P, COLS], F32, name="exp_alpha", bufs=4)
+            nc.scalar.activation(out=exp_alpha[t][:], in_=alpha_ps[:], func=ACT.Exp, bias=alpha_bias[:], scale=0.1)
+            bias2_ps = params(t, BIAS2)
+            bias2[t] = kept.tile([P, COLS], F32, name="bias2", bufs=4)
+            nc.scalar.activation(
+                out=bias2[t][:], in_=bias2_ps[:], func=ACT.Identity, bias=bias_one[:, 0:1], scale=1.0
+            )
+
+        def gate_products(t):
+            tanh_exp = kept.tile([P, COLS], F32)
+            nc.gpsimd.tensor_tensor(out=tanh_exp[:], in0=tanh_eps[t][:], in1=exp_alpha[t][:], op=ALU.mult)
+            x_scaled = kept.tile([P, COLS], F32)
+            nc.gpsimd.tensor_tensor(out=x_scaled[:], in0=exp_alpha[t][:], in1=turned[t][:, 1, :], op=ALU.mult)
+            gate_terms[t] = [tanh_exp, exp_alpha[t]]
+            base_terms[t] = [x_scaled, bias2[t]]
+
+        def log_denominator(t):
+            den_ps = transposed_sum([den_terms[t][:, l, :] for l in range(LS)])
+            log_den[t] = last.tile([P, COLS], F32, name="log_den")
+            nc.scalar.activation(out=log_den[t][:], in_=den_ps, func=ACT.Ln, bias=plus_one[:], scale=-1.0)
+
+        def inverse_denominator(t):
+            inv_den[t] = last.tile([P, COLS], F32, name="inv_den")
+            nc.scalar.activation(out=inv_den[t][:], in_=log_den[t][:], func=ACT.Exp, scale=-1.0)
+
+        def finish(t):
+            num_ps = transposed_sum(num_terms[t])
             ratio = last.tile([P, COLS], F32)
             nc.vector.scalar_tensor_tensor(
-                out=ratio[:], in0=num_ps[:].rearrange("p r d -> p (r d)"), scalar=0.4, in1=inv_den[:],
-                op0=ALU.mult, op1=ALU.mult,
+                out=ratio[:], in0=num_ps, scalar=0.4, in1=inv_den[t][:], op0=ALU.mult, op1=ALU.mult
             )
-            gate_ps = transposed_sum([gate])
+            gate_ps = transposed_sum(gate_terms[t])
             moved = last.tile([P, COLS], F32)
-            nc.vector.tensor_tensor(
-                out=moved[:], in0=gate_ps[:].rearrange("p r d -> p (r d)"), in1=ratio[:], op=ALU.mult
-            )
-            base_ps = transposed_sum([x_scaled, bias2])
+            nc.vector.tensor_tensor(out=moved[:], in0=gate_ps, in1=ratio[:], op=ALU.mult)
+            base_ps = transposed_sum(base_terms[t])
             result = last.tile([P, BLOCKS, DIM], F32)
             nc.vector.tensor_tensor(
-                out=result[:].rearrange("p r d -> p (r d)"),
-                in0=base_ps[:].rearrange("p r d -> p (r d)"),
-                in1=moved[:],
-                op=ALU.add,
+                out=result[:].rearrange("p r d -> p (r d)"), in0=base_ps, in1=moved[:], op=ALU.add
             )
-            nc.sync.dma_start(out=out_rows[:, block_rows, :], in_=result[:])
+            nc.sync.dma_start(out=out_rows[:, t * BLOCKS : (t + 1) * BLOCKS, :], in_=result[:])
+
+        for t in range(ROUNDS):
+            odd = t % 2 == 1
+            if t >= 1:
+                gate_products(t - 1)
+            for l in range(LS):
+                network_products(t, l)
+            denominator_terms(t)
+            if odd and t + 1 < ROUNDS:
+                for r in range(BLOCKS):
+                    hidden_block(t + 1, r)
+            if not odd and t >= 2:
+                inverse_denominator(t - 2)
+                inverse_denominator(t - 1)
+            for l in range(LS):
+                network_exp(t, l)
+            if not odd and t + 1 < ROUNDS:
+                for r in range(BLOCKS):
+                    hidden_block(t + 1, r)
+            gates(t)
+            for l in range(LS):
+                network_terms(t, l)
+            if t + 1 < ROUNDS:
+                quantise_hidden(t + 1)
+            if t >= 2:
+                finish(t - 2)
+            if t + 2 < ROUNDS:
+                turn(t + 2)
+            if odd:
+                log_denominator(t - 1)
+                log_denominator(t)
+        gate_products(ROUNDS - 1)
+        inverse_denominator(ROUNDS - 2)
+        inverse_denominator(ROUNDS - 1)
+        finish(ROUNDS - 2)
+        finish(ROUNDS - 1)

@@ -209,6 +209,9 @@ def tile_cn_pa_t_kernel(tc, x, cond, W1, b1, W2, b2, out):
         exp_alpha = {}
         bias2 = {}
         exp_z = {}
+        elu_plus_one = {}
+        ratio = {}
+        moved = {}
         num_terms = {}
         den_terms = {}
         gate_terms = {}
@@ -253,15 +256,17 @@ def tile_cn_pa_t_kernel(tc, x, cond, W1, b1, W2, b2, out):
                 out=exp_z[t, l][:], in_=z_plus_one[t, l][:], func=ACT.Exp, bias=minus_one[:], scale=1.0
             )
 
-        def network_terms(t, l):
-            elu_plus_one = work.tile([P, COLS], F32, bufs=2)
+        def network_elu(t, l):
+            elu_plus_one[t, l] = work.tile([P, COLS], F32, name="elu_plus_one")
             nc.vector.scalar_tensor_tensor(
-                out=elu_plus_one[:], in0=exp_z[t, l][:], scalar=1.0, in1=z_plus_one[t, l][:],
+                out=elu_plus_one[t, l][:], in0=exp_z[t, l][:], scalar=1.0, in1=z_plus_one[t, l][:],
                 op0=ALU.min, op1=ALU.max,
             )
+
+        def numerator_term(t, l):
             num_term = kept.tile([P, COLS], F32, bufs=4 * LS)
             nc.vector.scalar_tensor_tensor(
-                out=num_term[:], in0=elu_plus_one[:], scalar=-1.0, in1=mat2[t, l][:],
+                out=num_term[:], in0=elu_plus_one[t, l][:], scalar=-1.0, in1=mat2[t, l][:],
                 op0=ALU.add, op1=ALU.mult,
             )
             num_terms[t] = num_terms.get(t, []) + [num_term]
@@ -296,21 +301,27 @@ def tile_cn_pa_t_kernel(tc, x, cond, W1, b1, W2, b2, out):
             inv_den[t] = last.tile([P, COLS], F32, name="inv_den")
             nc.scalar.activation(out=inv_den[t][:], in_=log_den[t][:], func=ACT.Exp, scale=-1.0)
 
-        def finish(t):
+        def finish_ratio(t):
             num_ps = transposed_sum(num_terms[t])
-            ratio = last.tile([P, COLS], F32)
+            ratio[t] = last.tile([P, COLS], F32, name="ratio")
             nc.vector.scalar_tensor_tensor(
-                out=ratio[:], in0=num_ps, scalar=0.4, in1=inv_den[t][:], op0=ALU.mult, op1=ALU.mult
+                out=ratio[t][:], in0=num_ps, scalar=0.4, in1=inv_den[t][:], op0=ALU.mult, op1=ALU.mult
             )
+
+        def finish_gate(t):
             gate_ps = transposed_sum(gate_terms[t])
-            moved = last.tile([P, COLS], F32)
-            nc.vector.tensor_tensor(out=moved[:], in0=gate_ps, in1=ratio[:], op=ALU.mult)
+            moved[t] = last.tile([P, COLS], F32, name="moved")
+            nc.vector.tensor_tensor(out=moved[t][:], in0=gate_ps, in1=ratio[t][:], op=ALU.mult)
+
+        def finish_store(t):
             base_ps = transposed_sum(base_terms[t])
             result = last.tile([P, BLOCKS, DIM], F32)
             nc.vector.tensor_tensor(
-                out=result[:].rearrange("p r d -> p (r d)"), in0=base_ps, in1=moved[:], op=ALU.add
+                out=result[:].rearrange("p r d -> p (r d)"), in0=base_ps, in1=moved[t][:], op=ALU.add
             )
             nc.sync.dma_start(out=out_rows[:, t * BLOCKS : (t + 1) * BLOCKS, :], in_=result[:])
+
+        finish_steps = [finish_ratio, finish_gate, finish_store]
 
         for t in range(ROUNDS):
             odd = t % 2 == 1
@@ -319,31 +330,36 @@ def tile_cn_pa_t_kernel(tc, x, cond, W1, b1, W2, b2, out):
             for l in range(LS):
                 network_products(t, l)
             denominator_terms(t)
-            if odd and t + 1 < ROUNDS:
-                for r in range(BLOCKS):
-                    hidden_block(t + 1, r)
             if not odd and t >= 2:
                 inverse_denominator(t - 2)
                 inverse_denominator(t - 1)
-            for l in range(LS):
-                network_exp(t, l)
-            if not odd and t + 1 < ROUNDS:
+            if t + 1 < ROUNDS:
                 for r in range(BLOCKS):
                     hidden_block(t + 1, r)
-            gates(t)
+            if odd:
+                gates(t)
+                if t + 2 < ROUNDS:
+                    turn(t + 2)
             for l in range(LS):
-                network_terms(t, l)
+                network_exp(t, l)
+                if t >= 2:
+                    finish_steps[l](t - 2)
+            if not odd:
+                gates(t)
+                if t + 2 < ROUNDS:
+                    turn(t + 2)
             if t + 1 < ROUNDS:
                 quantise_hidden(t + 1)
-            if t >= 2:
-                finish(t - 2)
-            if t + 2 < ROUNDS:
-                turn(t + 2)
+            for l in range(LS):
+                network_elu(t, l)
+            for l in range(LS):
+                numerator_term(t, l)
             if odd:
                 log_denominator(t - 1)
                 log_denominator(t)
         gate_products(ROUNDS - 1)
         inverse_denominator(ROUNDS - 2)
         inverse_denominator(ROUNDS - 1)
-        finish(ROUNDS - 2)
-        finish(ROUNDS - 1)
+        for step in finish_steps:
+            step(ROUNDS - 2)
+            step(ROUNDS - 1)

@@ -285,11 +285,15 @@ def tile_cn_pa_t_kernel(tc, x, cond, W1, b1, W2, b2, out):
             )
 
         def gate_products(t):
-            tanh_exp = kept.tile([P, COLS], F32)
-            nc.gpsimd.tensor_tensor(out=tanh_exp[:], in0=tanh_eps[t][:], in1=exp_alpha[t][:], op=ALU.mult)
+            sigmoid_eps = kept.tile([P, COLS], F32)
+            nc.gpsimd.tensor_scalar(
+                out=sigmoid_eps[:], in0=tanh_eps[t][:], scalar1=1.0, scalar2=0.4, op0=ALU.add, op1=ALU.mult
+            )
+            gate = kept.tile([P, COLS], F32)
+            nc.gpsimd.tensor_tensor(out=gate[:], in0=sigmoid_eps[:], in1=exp_alpha[t][:], op=ALU.mult)
             x_scaled = kept.tile([P, COLS], F32)
             nc.gpsimd.tensor_tensor(out=x_scaled[:], in0=exp_alpha[t][:], in1=turned[t][:, 1, :], op=ALU.mult)
-            gate_terms[t] = [tanh_exp, exp_alpha[t]]
+            gate_terms[t] = [gate]
             base_terms[t] = [x_scaled, bias2[t]]
 
         def log_denominator(t):
@@ -304,9 +308,7 @@ def tile_cn_pa_t_kernel(tc, x, cond, W1, b1, W2, b2, out):
         def finish_ratio(t):
             num_ps = transposed_sum(num_terms[t])
             ratio[t] = last.tile([P, COLS], F32, name="ratio")
-            nc.vector.scalar_tensor_tensor(
-                out=ratio[t][:], in0=num_ps, scalar=0.4, in1=inv_den[t][:], op0=ALU.mult, op1=ALU.mult
-            )
+            nc.vector.tensor_tensor(out=ratio[t][:], in0=num_ps, in1=inv_den[t][:], op=ALU.mult)
 
         def finish_gate(t):
             gate_ps = transposed_sum(gate_terms[t])

@@ -202,6 +202,7 @@ def tile_cn_pa_t_kernel(tc, x, cond, W1, b1, W2, b2, out):
             return total[:].rearrange("p r d -> p (r d)")
 
         mat2 = {}
+        base_ps = {}
         z_plus_one = {}
         mat1_mat2 = {}
         x_mat1 = {}
@@ -315,15 +316,16 @@ def tile_cn_pa_t_kernel(tc, x, cond, W1, b1, W2, b2, out):
             moved[t] = last.tile([P, COLS], F32, name="moved")
             nc.vector.tensor_tensor(out=moved[t][:], in0=gate_ps, in1=ratio[t][:], op=ALU.mult)
 
+        def finish_base(t):
+            base_ps[t] = transposed_sum(base_terms[t])
+
         def finish_store(t):
-            base_ps = transposed_sum(base_terms[t])
             result = last.tile([P, BLOCKS, DIM], F32)
             nc.vector.tensor_tensor(
-                out=result[:].rearrange("p r d -> p (r d)"), in0=base_ps, in1=moved[t][:], op=ALU.add
+                out=result[:].rearrange("p r d -> p (r d)"), in0=base_ps[t], in1=moved[t][:], op=ALU.add
             )
             nc.sync.dma_start(out=out_rows[:, t * BLOCKS : (t + 1) * BLOCKS, :], in_=result[:])
 
-        finish_steps = [finish_ratio, finish_gate, finish_store]
 
         for t in range(ROUNDS):
             odd = t % 2 == 1
@@ -342,16 +344,22 @@ def tile_cn_pa_t_kernel(tc, x, cond, W1, b1, W2, b2, out):
                 gates(t)
                 if t + 2 < ROUNDS:
                     turn(t + 2)
-            for l in range(LS):
-                network_exp(t, l)
-                if t >= 2:
-                    finish_steps[l](t - 2)
+            network_exp(t, 0)
+            network_exp(t, 1)
+            if t >= 2:
+                finish_ratio(t - 2)
+            network_exp(t, 2)
+            if t >= 2:
+                finish_gate(t - 2)
+                finish_base(t - 2)
             if not odd:
                 gates(t)
                 if t + 2 < ROUNDS:
                     turn(t + 2)
             if t + 1 < ROUNDS:
                 quantise_hidden(t + 1)
+            if t >= 2:
+                finish_store(t - 2)
             for l in range(LS):
                 network_elu(t, l)
             for l in range(LS):
@@ -362,6 +370,6 @@ def tile_cn_pa_t_kernel(tc, x, cond, W1, b1, W2, b2, out):
         gate_products(ROUNDS - 1)
         inverse_denominator(ROUNDS - 2)
         inverse_denominator(ROUNDS - 1)
-        for step in finish_steps:
+        for step in (finish_ratio, finish_gate, finish_base, finish_store):
             step(ROUNDS - 2)
             step(ROUNDS - 1)

@@ -342,8 +342,6 @@ def tile_cn_pa_t_kernel(tc, x, cond, W1, b1, W2, b2, out):
                     hidden_block(t + 1, r)
             if odd:
                 gates(t)
-                if t + 2 < ROUNDS:
-                    turn(t + 2)
             network_exp(t, 0)
             network_exp(t, 1)
             if t >= 2:
@@ -354,8 +352,8 @@ def tile_cn_pa_t_kernel(tc, x, cond, W1, b1, W2, b2, out):
                 finish_base(t - 2)
             if not odd:
                 gates(t)
-                if t + 2 < ROUNDS:
-                    turn(t + 2)
+            if t + 2 < ROUNDS:
+                turn(t + 2)
             if t + 1 < ROUNDS:
                 quantise_hidden(t + 1)
             if t >= 2:

@@ -21,17 +21,18 @@ PARAMS = 1536
 COLS = 512
 BLOCKS = COLS // P
 ROUNDS = BATCH // COLS
+SLOTS = ROUNDS * LS
 ROWS_PER_PARTITION = BATCH // P
-CHUNKS = PARAMS // P
 SECTION = LS * DIM
-MAT1 = 0
-BIAS1 = 1
-MAT2 = 2
-BIAS2 = 9
-EPS = 10
-ALPHA = 11
-PSUM_BANKS = 8
+MAT1, BIAS1, MAT2 = 0, 1, 2
+BIAS2, EPS, ALPHA = 0, 1, 2
+MATMUL_BIAS_ROUNDS = 5
 LOWEST = -3.0e38
+CHUNKS = (
+    (MAT2, 0), (MAT1, 0), (BIAS1, 0), (MAT2, 1),
+    (MAT1, 1), (BIAS1, 1), (MAT2, 2), (MAT1, 2),
+    (BIAS1, 2), (3, BIAS2), (3, EPS), (3, ALPHA),
+)
 
 FLOPS = 2 * BATCH * DIM * HID + 2 * BATCH * HID * PARAMS
 
@@ -46,44 +47,53 @@ def tile_cn_pa_t_kernel(tc, x, cond, W1, b1, W2, b2, out):
         ctx.enter_context(tc.manual_schedule())
         consts = ctx.enter_context(tc.tile_pool(name="consts", bufs=1))
         rows = ctx.enter_context(tc.tile_pool(name="rows", bufs=ROUNDS))
-        hidden = ctx.enter_context(tc.tile_pool(name="hidden", bufs=2))
-        work = ctx.enter_context(tc.tile_pool(name="work", bufs=LS + 1))
+        hidden = ctx.enter_context(tc.tile_pool(name="hidden", bufs=3))
+        work = ctx.enter_context(tc.tile_pool(name="work", bufs=3))
         kept = ctx.enter_context(tc.tile_pool(name="kept", bufs=3))
         last = ctx.enter_context(tc.tile_pool(name="last", bufs=2))
-        psum = ctx.enter_context(tc.psum_pool(name="psum", bufs=PSUM_BANKS))
+        psum = ctx.enter_context(tc.psum_pool(name="psum", bufs=1))
 
-        def bank(shape, dtype):
-            return psum.tile(shape, dtype, name="bank", tag="bank")
+        def vector_bank(shape, dtype):
+            return psum.tile(shape, dtype, name="vector_bank", tag="vector_bank", bufs=4)
+
+        def scalar_bank(shape, dtype):
+            return psum.tile(shape, dtype, name="scalar_bank", tag="scalar_bank", bufs=3)
+
+        def sum_bank(shape, dtype):
+            return psum.tile(shape, dtype, name="sum_bank", tag="sum_bank", bufs=1)
 
         cond_t = {}
         x_t = {}
 
-        def load_rows(t):
-            block_rows = slice(t * BLOCKS, (t + 1) * BLOCKS)
-            cond_t[t] = rows.tile([P, BLOCKS, DIM], BF16, name="cond_t")
-            nc.sync.dma_start(out=cond_t[t][:], in_=cond_rows[:, block_rows, :])
-            x_t[t] = rows.tile([P, BLOCKS, DIM], BF16, name="x_t")
-            nc.sync.dma_start(out=x_t[t][:], in_=x_rows[:, block_rows, :])
+        def load_rows(t, which, name, source):
+            which[t] = rows.tile([P, BLOCKS, DIM], BF16, name=name)
+            nc.sync.dma_start(out=which[t][:], in_=source[:, t * BLOCKS : (t + 1) * BLOCKS, :])
 
         w1_sb = consts.tile([P, HID], BF16)
         nc.sync.dma_start(out=w1_sb[:], in_=W1)
         b1_row = consts.tile([P, HID], BF16)
         nc.vector.memset(b1_row[:], 0.0)
+        b2_row = consts.tile([P, SECTION], BF16)
+        nc.vector.memset(b2_row[:], 0.0)
+        load_rows(0, cond_t, "cond_t", cond_rows)
         nc.sync.dma_start(out=b1_row[0:1, :], in_=b1.rearrange("(o k) -> o k", o=1))
-        load_rows(0)
+        nc.sync.dma_start(out=b2_row[0:4, :], in_=b2.rearrange("(s c) -> s c", s=4))
         w2_rows = W2.rearrange("(p j) c -> p j c", j=PACK)
-        w2_raw = []
-        for s in range(4):
-            w2_part = consts.tile([P, PACK, SECTION], BF16, name="w2_raw%d" % s)
-            nc.sync.dma_start(out=w2_part[:], in_=w2_rows[:, :, s * SECTION : (s + 1) * SECTION])
-            w2_raw.append(w2_part)
-        b2_ls_bf = consts.tile([P, 3, LS], BF16)
-        b2_one_bf = consts.tile([P, 3], BF16)
-        with nc.allow_non_contiguous_dma(reason="a bias vector, one feature to a partition"):
-            nc.sync.dma_start(out=b2_ls_bf[:], in_=b2[0 : 3 * SECTION].rearrange("(s d l) -> d s l", s=3, l=LS))
-            nc.sync.dma_start(out=b2_one_bf[:], in_=b2[3 * SECTION : PARAMS].rearrange("(s d) -> d s", s=3))
-        for t in range(1, ROUNDS):
-            load_rows(t)
+        w2_raw = {}
+
+        def load_w2(s):
+            w2_raw[s] = consts.tile([P, PACK, SECTION], BF16, name="w2_raw%d" % s)
+            nc.sync.dma_start(out=w2_raw[s][:], in_=w2_rows[:, :, s * SECTION : (s + 1) * SECTION])
+
+        for s in (MAT2, MAT1, BIAS1):
+            load_w2(s)
+        load_rows(0, x_t, "x_t", x_rows)
+        load_rows(1, cond_t, "cond_t", cond_rows)
+        load_rows(1, x_t, "x_t", x_rows)
+        load_w2(3)
+        for t in range(2, ROUNDS):
+            load_rows(t, cond_t, "cond_t", cond_rows)
+            load_rows(t, x_t, "x_t", x_rows)
 
         ident_bf = consts.tile([P, P], BF16)
         make_identity(nc, ident_bf[:])
@@ -93,37 +103,54 @@ def tile_cn_pa_t_kernel(tc, x, cond, W1, b1, W2, b2, out):
         nc.vector.memset(minus_one[:], -1.0)
         plus_one = consts.tile([P, 1], F32)
         nc.vector.memset(plus_one[:], 1.0)
-        w1_r = consts.tile([P, PACK, P], BF16)
-        nc.vector.tensor_copy(out=w1_r[:], in_=w1_sb[:].rearrange("d (p j) -> d j p", j=PACK))
         ones = consts.tile([P, P], BF16)
         nc.vector.memset(ones[:], 1.0)
-        b1_ps = bank([P, HID], F32)
-        nc.tensor.matmul(out=b1_ps[:], lhsT=ones[:], rhs=b1_row[:], start=True, stop=True)
-        b1_rows = consts.tile([P, PACK, P], F32)
-        nc.vector.tensor_copy(out=b1_rows[:], in_=b1_ps[:].rearrange("w (p j) -> w j p", j=PACK))
+        w1_r = consts.tile([P, PACK, P], BF16)
+        nc.vector.tensor_copy(out=w1_r[:], in_=w1_sb[:].rearrange("d (p j) -> d j p", j=PACK))
 
         turned = {}
         grouped = {}
         h_codes = {}
         h_scales = {}
 
-        def turn(t):
-            turned_ps = bank([P, 2, COLS], BF16)
-            for r in range(BLOCKS):
-                nc.tensor.transpose(turned_ps[:, 0, r * P : (r + 1) * P], cond_t[t][:, r, :], ident_bf[:])
-            for r in range(BLOCKS):
-                nc.tensor.transpose(turned_ps[:, 1, r * P : (r + 1) * P], x_t[t][:, r, :], ident_bf[:])
-            turned[t] = hidden.tile([P, 2, COLS], BF16, name="turned", bufs=3)
-            nc.scalar.copy(out=turned[t][:], in_=turned_ps[:])
+        def turn(t, parts):
+            if t not in turned:
+                turned[t] = hidden.tile([P, 2, COLS], BF16, name="turned", bufs=5)
+            turned_ps = scalar_bank([P, 2, COLS], BF16)
+            for part in parts:
+                source = (cond_t, x_t)[part][t]
+                for r in range(BLOCKS):
+                    nc.tensor.transpose(turned_ps[:, part, r * P : (r + 1) * P], source[:, r, :], ident_bf[:])
+            part_range = slice(parts[0], parts[-1] + 1)
+            nc.scalar.copy(out=turned[t][:, part_range, :], in_=turned_ps[:, part_range, :])
 
+        turn(0, (0,))
+        b2_ps = vector_bank([P, 2 * LS, P], BF16)
+        for l in range(LS):
+            nc.tensor.transpose(b2_ps[:, l, :], b2_row[:, l:SECTION:LS], ident_bf[:])
+        for part in range(LS):
+            nc.tensor.transpose(b2_ps[:, LS + part, :], b2_row[:, part * P : (part + 1) * P], ident_bf[:])
+        bias = consts.tile([P, 2 * LS, 4], F32)
+        nc.vector.tensor_copy(out=bias[:], in_=b2_ps[:, :, 0:4])
+        bias1_plus_one = consts.tile([P, LS], F32)
+        nc.vector.tensor_scalar_add(out=bias1_plus_one[:], in0=bias[:, 0:LS, BIAS1], scalar1=1.0)
+        eps_bias = consts.tile([P, 1], F32)
+        nc.vector.tensor_scalar_mul(out=eps_bias[:], in0=bias[:, LS + EPS, 3:4], scalar1=0.05)
+        alpha_bias = consts.tile([P, 1], F32)
+        nc.vector.tensor_scalar_mul(out=alpha_bias[:], in0=bias[:, LS + ALPHA, 3:4], scalar1=0.1)
+        b1_planes = consts.tile([P, PACK, P], BF16)
+        nc.vector.tensor_copy(out=b1_planes[:], in_=b1_row[:].rearrange("o (p j) -> o j p", j=PACK))
         def hidden_block(t, r):
             if r == 0:
                 grouped[t] = hidden.tile([P, COLS, PACK], BF16, name="grouped", align_bytes=64)
-            h_ps = bank([P, PACK, P], F32)
+            h_ps = scalar_bank([P, PACK, P], F32)
             for j in range(PACK):
-                nc.tensor.matmul(
-                    out=h_ps[:, j, :], lhsT=b1_rows[:, j, :], rhs=ident_f[:], is_transpose=True, start=True, stop=False
-                )
+                if t < MATMUL_BIAS_ROUNDS:
+                    nc.tensor.matmul(out=h_ps[:, j, :], lhsT=b1_planes[:, j, :], rhs=ones[:], start=True, stop=False)
+                else:
+                    nc.tensor.matmul(
+                        out=h_ps[:, j, :], lhsT=b1_rows[:, j, :], rhs=ident_f[:], is_transpose=True, start=True, stop=False
+                    )
                 nc.tensor.matmul(
                     out=h_ps[:, j, :], lhsT=w1_r[:, j, :], rhs=turned[t][:, 0, r * P : (r + 1) * P],
                     start=False, stop=True,
@@ -141,45 +168,30 @@ def tile_cn_pa_t_kernel(tc, x, cond, W1, b1, W2, b2, out):
                 in_=grouped[t][:].rearrange("p w j -> p (w j)"),
             )
 
-        turn(0)
-        for r in range(BLOCKS):
-            hidden_block(0, r)
-        turn(1)
+        w2_grp = consts.tile([P, len(CHUNKS), P, PACK], BF16, align_bytes=64)
+        w2_codes = consts.tile([P, len(CHUNKS), P], U32, align_bytes=64)
+        w2_scales = consts.tile([P, len(CHUNKS), P], U8, align_bytes=64)
 
-        w2_grp = consts.tile([P, CHUNKS, P, PACK], BF16, align_bytes=64)
-        for s in range(3):
+        def group_chunk(c):
+            s, l = CHUNKS[c]
             nc.vector.tensor_copy(
-                out=w2_grp[:, s * LS : (s + 1) * LS, :, :], in_=w2_raw[s][:].rearrange("p j (d l) -> p l d j", l=LS)
+                out=w2_grp[:, c, :, :], in_=w2_raw[s][:].rearrange("p j (d l) -> p l d j", l=LS)[:, l, :, :]
             )
-        quantise_hidden(0)
-        nc.vector.tensor_copy(
-            out=w2_grp[:, BIAS2:CHUNKS, :, :], in_=w2_raw[3][:].rearrange("p j (s d) -> p s d j", s=3)
-        )
-        w2_codes = consts.tile([P, CHUNKS, P], U32, align_bytes=64)
-        w2_scales = consts.tile([P, CHUNKS, P], U8, align_bytes=64)
-        for c in range(0, CHUNKS, 4):
+
+        def quantise_chunks(c):
             nc.vector.quantize_mx(
                 out=w2_codes[:, c : c + 4, :].rearrange("p c d -> p (c d)").bitcast(FP8X4),
                 scales=w2_scales[:, c : c + 4, :].rearrange("p c d -> p (c d)"),
                 in_=w2_grp[:, c : c + 4, :, :].rearrange("p c d j -> p (c d j)"),
             )
-        bias_ls = consts.tile([P, 3, LS], F32)
-        nc.vector.tensor_copy(out=bias_ls[:], in_=b2_ls_bf[:])
-        bias1_plus_one = consts.tile([P, LS], F32)
-        nc.vector.tensor_scalar_add(out=bias1_plus_one[:], in0=bias_ls[:, BIAS1, :], scalar1=1.0)
-        bias_one = consts.tile([P, 3], F32)
-        nc.vector.tensor_copy(out=bias_one[:], in_=b2_one_bf[:])
-        eps_bias = consts.tile([P, 1], F32)
-        nc.vector.tensor_scalar_mul(out=eps_bias[:], in0=bias_one[:, 1:2], scalar1=0.05)
-        alpha_bias = consts.tile([P, 1], F32)
-        nc.vector.tensor_scalar_mul(out=alpha_bias[:], in0=bias_one[:, 2:3], scalar1=0.1)
 
-        def params(t, chunk):
+        def params(t, section, part, bank):
+            c = CHUNKS.index((section, part))
             p_ps = bank([P, COLS], F32)
             nc.tensor.matmul_mx(
                 out=p_ps[:],
-                lhsT=w2_codes[:, chunk, :].bitcast(FP8X4),
-                lhsT_scale=w2_scales[:, chunk, :],
+                lhsT=w2_codes[:, c, :].bitcast(FP8X4),
+                lhsT_scale=w2_scales[:, c, :],
                 rhs=h_codes[t][:].bitcast(FP8X4),
                 rhs_scale=h_scales[t][:],
                 start=True,
@@ -187,7 +199,7 @@ def tile_cn_pa_t_kernel(tc, x, cond, W1, b1, W2, b2, out):
             )
             return p_ps
 
-        def transposed_sum(terms):
+        def transposed_sum(terms, bank):
             total = bank([P, BLOCKS, P], F32)
             for r in range(BLOCKS):
                 for i, term in enumerate(terms):
@@ -202,103 +214,120 @@ def tile_cn_pa_t_kernel(tc, x, cond, W1, b1, W2, b2, out):
             return total[:].rearrange("p r d -> p (r d)")
 
         mat2 = {}
-        base_ps = {}
-        z_plus_one = {}
-        mat1_mat2 = {}
+        mat1_ps = {}
+        bias1_ps = {}
+        den_term = {}
         x_mat1 = {}
+        z_plus_one = {}
+        exp_z = {}
+        elu_plus_one = {}
+        num_term = {}
         tanh_eps = {}
         exp_alpha = {}
         bias2 = {}
-        exp_z = {}
-        elu_plus_one = {}
-        ratio = {}
-        moved = {}
-        num_terms = {}
-        den_terms = {}
-        gate_terms = {}
-        base_terms = {}
+        sigmoid_eps = {}
+        gate = {}
+        x_scaled = {}
         log_den = {}
         inv_den = {}
+        ratio = {}
+        moved = {}
+        sums = {}
 
-        def network_products(t, l):
-            mat2_ps = params(t, MAT2 * LS + l)
-            mat2[t, l] = work.tile([P, COLS], F32, name="mat2")
+        def mat2_pass(g):
+            t, l = divmod(g, LS)
+            mat2_ps = params(t, MAT2, l, scalar_bank)
+            mat2[g] = work.tile([P, COLS], F32, name="mat2", bufs=5)
             nc.scalar.activation(
-                out=mat2[t, l][:], in_=mat2_ps[:], func=ACT.Identity, bias=bias_ls[:, MAT2, l : l + 1], scale=1.0
+                out=mat2[g][:], in_=mat2_ps[:], func=ACT.Identity, bias=bias[:, l, MAT2 : MAT2 + 1], scale=1.0
             )
-            mat1_ps = params(t, MAT1 * LS + l)
-            if l == 0:
-                mat1_mat2[t] = work.tile([P, LS, COLS], F32, name="mat1_mat2", bufs=2)
+
+        def mat1_pass(g):
+            t, l = divmod(g, LS)
+            mat1_ps[g] = params(t, MAT1, l, vector_bank)
+
+        def bias1_pass(g):
+            t, l = divmod(g, LS)
+            bias1_ps[g] = params(t, BIAS1, l, vector_bank)
+
+        def x_product(g):
+            t, l = divmod(g, LS)
+            x_mat1[g] = work.tile([P, COLS], F32, name="x_mat1")
             nc.vector.scalar_tensor_tensor(
-                out=mat1_mat2[t][:, l, :], in0=mat1_ps[:], scalar=bias_ls[:, MAT1, l : l + 1], in1=mat2[t, l][:],
-                op0=ALU.add, op1=ALU.mult,
-            )
-            x_mat1[t, l] = work.tile([P, COLS], F32, name="x_mat1")
-            nc.vector.scalar_tensor_tensor(
-                out=x_mat1[t, l][:], in0=mat1_ps[:], scalar=bias_ls[:, MAT1, l : l + 1], in1=turned[t][:, 1, :],
+                out=x_mat1[g][:], in0=mat1_ps[g][:], scalar=bias[:, l, MAT1 : MAT1 + 1], in1=turned[t][:, 1, :],
                 op0=ALU.add, op1=ALU.mult,
             )
 
-        def denominator_terms(t):
-            den_terms[t] = kept.tile([P, LS, COLS], F32, name="den_terms")
+        def mat_product(g):
+            t, l = divmod(g, LS)
+            den_term[g] = kept.tile([P, COLS], F32, name="den_term", bufs=9)
+            nc.vector.scalar_tensor_tensor(
+                out=den_term[g][:], in0=mat1_ps[g][:], scalar=bias[:, l, MAT1 : MAT1 + 1], in1=mat2[g][:],
+                op0=ALU.add, op1=ALU.mult,
+            )
             nc.gpsimd.tensor_scalar(
-                out=den_terms[t][:], in0=mat1_mat2[t][:], scalar1=0.0, scalar2=LOWEST, op0=ALU.min, op1=ALU.max
+                out=den_term[g][:], in0=den_term[g][:], scalar1=0.0, scalar2=LOWEST, op0=ALU.min, op1=ALU.max
             )
 
-        def network_exp(t, l):
-            bias1_ps = params(t, BIAS1 * LS + l)
-            z_plus_one[t, l] = work.tile([P, COLS], F32, name="z_plus_one")
+        def z_step(g):
+            l = g % LS
+            z_plus_one[g] = work.tile([P, COLS], F32, name="z_plus_one")
             nc.vector.scalar_tensor_tensor(
-                out=z_plus_one[t, l][:], in0=bias1_ps[:], scalar=bias1_plus_one[:, l : l + 1], in1=x_mat1[t, l][:],
+                out=z_plus_one[g][:], in0=bias1_ps[g][:], scalar=bias1_plus_one[:, l : l + 1], in1=x_mat1[g][:],
                 op0=ALU.add, op1=ALU.add,
             )
-            exp_z[t, l] = work.tile([P, COLS], F32, name="exp_z")
+
+        def exp_step(g):
+            exp_z[g] = work.tile([P, COLS], F32, name="exp_z")
             nc.scalar.activation(
-                out=exp_z[t, l][:], in_=z_plus_one[t, l][:], func=ACT.Exp, bias=minus_one[:], scale=1.0
+                out=exp_z[g][:], in_=z_plus_one[g][:], func=ACT.Exp, bias=minus_one[:], scale=1.0
             )
 
-        def network_elu(t, l):
-            elu_plus_one[t, l] = work.tile([P, COLS], F32, name="elu_plus_one")
+        def elu_step(g):
+            elu_plus_one[g] = work.tile([P, COLS], F32, name="elu_plus_one")
             nc.vector.scalar_tensor_tensor(
-                out=elu_plus_one[t, l][:], in0=exp_z[t, l][:], scalar=1.0, in1=z_plus_one[t, l][:],
-                op0=ALU.min, op1=ALU.max,
+                out=elu_plus_one[g][:], in0=exp_z[g][:], scalar=1.0, in1=z_plus_one[g][:], op0=ALU.min, op1=ALU.max,
             )
 
-        def numerator_term(t, l):
-            num_term = kept.tile([P, COLS], F32, bufs=4 * LS)
+        def term_step(g):
+            num_term[g] = kept.tile([P, COLS], F32, name="num_term", bufs=9)
             nc.vector.scalar_tensor_tensor(
-                out=num_term[:], in0=elu_plus_one[t, l][:], scalar=-1.0, in1=mat2[t, l][:],
-                op0=ALU.add, op1=ALU.mult,
+                out=num_term[g][:], in0=elu_plus_one[g][:], scalar=-1.0, in1=mat2[g][:], op0=ALU.add, op1=ALU.mult,
             )
-            num_terms[t] = num_terms.get(t, []) + [num_term]
 
-        def gates(t):
-            eps_ps = params(t, EPS)
-            tanh_eps[t] = kept.tile([P, COLS], F32, name="tanh_eps")
-            nc.scalar.activation(out=tanh_eps[t][:], in_=eps_ps[:], func=ACT.Tanh, bias=eps_bias[:], scale=0.05)
-            alpha_ps = params(t, ALPHA)
-            exp_alpha[t] = kept.tile([P, COLS], F32, name="exp_alpha", bufs=4)
-            nc.scalar.activation(out=exp_alpha[t][:], in_=alpha_ps[:], func=ACT.Exp, bias=alpha_bias[:], scale=0.1)
-            bias2_ps = params(t, BIAS2)
+        def bias2_pass(t):
+            ps = params(t, 3, BIAS2, scalar_bank)
             bias2[t] = kept.tile([P, COLS], F32, name="bias2", bufs=4)
             nc.scalar.activation(
-                out=bias2[t][:], in_=bias2_ps[:], func=ACT.Identity, bias=bias_one[:, 0:1], scale=1.0
+                out=bias2[t][:], in_=ps[:], func=ACT.Identity, bias=bias[:, LS + BIAS2, 3:4], scale=1.0
             )
 
-        def gate_products(t):
-            sigmoid_eps = kept.tile([P, COLS], F32)
+        def eps_pass(t):
+            ps = params(t, 3, EPS, scalar_bank)
+            tanh_eps[t] = kept.tile([P, COLS], F32, name="tanh_eps", bufs=3)
+            nc.scalar.activation(out=tanh_eps[t][:], in_=ps[:], func=ACT.Tanh, bias=eps_bias[:], scale=0.05)
+
+        def alpha_pass(t):
+            ps = params(t, 3, ALPHA, scalar_bank)
+            exp_alpha[t] = kept.tile([P, COLS], F32, name="exp_alpha", bufs=4)
+            nc.scalar.activation(out=exp_alpha[t][:], in_=ps[:], func=ACT.Exp, bias=alpha_bias[:], scale=0.1)
+
+        def sigmoid_step(t):
+            sigmoid_eps[t] = kept.tile([P, COLS], F32, name="sigmoid_eps", bufs=2)
             nc.gpsimd.tensor_scalar(
-                out=sigmoid_eps[:], in0=tanh_eps[t][:], scalar1=1.0, scalar2=0.4, op0=ALU.add, op1=ALU.mult
+                out=sigmoid_eps[t][:], in0=tanh_eps[t][:], scalar1=1.0, scalar2=0.4, op0=ALU.add, op1=ALU.mult
             )
-            gate = kept.tile([P, COLS], F32)
-            nc.gpsimd.tensor_tensor(out=gate[:], in0=sigmoid_eps[:], in1=exp_alpha[t][:], op=ALU.mult)
-            x_scaled = kept.tile([P, COLS], F32)
-            nc.gpsimd.tensor_tensor(out=x_scaled[:], in0=exp_alpha[t][:], in1=turned[t][:, 1, :], op=ALU.mult)
-            gate_terms[t] = [gate]
-            base_terms[t] = [x_scaled, bias2[t]]
+
+        def gate_step(t):
+            gate[t] = kept.tile([P, COLS], F32, name="gate", bufs=3)
+            nc.gpsimd.tensor_tensor(out=gate[t][:], in0=sigmoid_eps[t][:], in1=exp_alpha[t][:], op=ALU.mult)
+
+        def x_scaled_step(t):
+            x_scaled[t] = kept.tile([P, COLS], F32, name="x_scaled", bufs=3)
+            nc.gpsimd.tensor_tensor(out=x_scaled[t][:], in0=exp_alpha[t][:], in1=turned[t][:, 1, :], op=ALU.mult)
 
         def log_denominator(t):
-            den_ps = transposed_sum([den_terms[t][:, l, :] for l in range(LS)])
+            den_ps = transposed_sum([den_term[LS * t + l] for l in range(LS)], scalar_bank)
             log_den[t] = last.tile([P, COLS], F32, name="log_den")
             nc.scalar.activation(out=log_den[t][:], in_=den_ps, func=ACT.Ln, bias=plus_one[:], scale=-1.0)
 
@@ -306,68 +335,177 @@ def tile_cn_pa_t_kernel(tc, x, cond, W1, b1, W2, b2, out):
             inv_den[t] = last.tile([P, COLS], F32, name="inv_den")
             nc.scalar.activation(out=inv_den[t][:], in_=log_den[t][:], func=ACT.Exp, scale=-1.0)
 
-        def finish_ratio(t):
-            num_ps = transposed_sum(num_terms[t])
-            ratio[t] = last.tile([P, COLS], F32, name="ratio")
-            nc.vector.tensor_tensor(out=ratio[t][:], in0=num_ps, in1=inv_den[t][:], op=ALU.mult)
-
-        def finish_gate(t):
-            gate_ps = transposed_sum(gate_terms[t])
-            moved[t] = last.tile([P, COLS], F32, name="moved")
-            nc.vector.tensor_tensor(out=moved[t][:], in0=gate_ps, in1=ratio[t][:], op=ALU.mult)
-
-        def finish_base(t):
-            base_ps[t] = transposed_sum(base_terms[t])
-
-        def finish_store(t):
-            result = last.tile([P, BLOCKS, DIM], F32)
-            nc.vector.tensor_tensor(
-                out=result[:].rearrange("p r d -> p (r d)"), in0=base_ps[t], in1=moved[t][:], op=ALU.add
+        def finish_sum(step, t, bank):
+            terms = (
+                [num_term[LS * t + l] for l in range(LS)] if step == 0 else [gate[t]] if step == 1 else [x_scaled[t], bias2[t]]
             )
-            nc.sync.dma_start(out=out_rows[:, t * BLOCKS : (t + 1) * BLOCKS, :], in_=result[:])
+            sums[step, t] = transposed_sum(terms, bank)
 
+        def finish(step, t):
+            if step == 0:
+                ratio[t] = last.tile([P, COLS], F32, name="ratio")
+                nc.vector.tensor_tensor(out=ratio[t][:], in0=sums[0, t], in1=inv_den[t][:], op=ALU.mult)
+            elif step == 1:
+                moved[t] = last.tile([P, COLS], F32, name="moved")
+                nc.vector.tensor_tensor(out=moved[t][:], in0=sums[1, t], in1=ratio[t][:], op=ALU.mult)
+            else:
+                result = last.tile([P, BLOCKS, DIM], F32, name="result")
+                nc.vector.tensor_tensor(
+                    out=result[:].rearrange("p r d -> p (r d)"), in0=sums[2, t], in1=moved[t][:], op=ALU.add
+                )
+                nc.sync.dma_start(out=out_rows[:, t * BLOCKS : (t + 1) * BLOCKS, :], in_=result[:])
 
-        for t in range(ROUNDS):
-            odd = t % 2 == 1
+        for r in range(BLOCKS):
+            hidden_block(0, r)
+        turn(0, (1,))
+        for c in range(4):
+            group_chunk(c)
+        quantise_chunks(0)
+        for c in range(4, 6):
+            group_chunk(c)
+        quantise_hidden(0)
+        turn(1, (0, 1))
+        hidden_block(1, 0)
+        mat2_pass(0)
+        mat1_pass(0)
+        bias1_pass(0)
+        for part in range(LS):
+            nc.gpsimd.tensor_scalar(
+                out=w2_grp[:, 9 + part, :, :], in0=w2_raw[3][:].rearrange("p j (s d) -> p s d j", s=LS)[:, part, :, :],
+                scalar1=1.0, scalar2=0.0, op0=ALU.mult, op1=ALU.add,
+            )
+        for c in range(6, 8):
+            group_chunk(c)
+        x_product(0)
+        quantise_chunks(4)
+        b1_ps = scalar_bank([P, HID], F32)
+        nc.tensor.matmul(out=b1_ps[:], lhsT=ones[:], rhs=b1_row[:], start=True, stop=True)
+        b1_rows = consts.tile([P, PACK, P], F32)
+        nc.vector.tensor_copy(out=b1_rows[:], in_=b1_ps[:].rearrange("w (p j) -> w j p", j=PACK))
+
+        turns = {1: 2, 2: 3}
+        blocks = {0: [(1, 1), (1, 2)], 1: [(1, 3)], 2: [(2, 0), (2, 1), (2, 2)], 3: [(2, 3), (3, 0)], 4: [(3, 1), (3, 2)], 5: [(3, 3)]}
+        for t in range(4, ROUNDS):
+            turns[LS * (t - 2) - 1] = t
+            for l in (0, 1):
+                blocks[LS * (t - 2) + l] = [(t, 2 * l), (t, 2 * l + 1)]
+        quantise_at = {2: 1}
+        for t in range(2, ROUNDS):
+            quantise_at[LS * (t - 1) + 1] = t
+
+        first_finish = 7
+
+        def finish_of(g):
+            if g < first_finish:
+                return None
+            t, step = divmod(g - first_finish, LS)
+            return step, t
+
+        for g in range(SLOTS - LS):
+            t, l = divmod(g, LS)
+            if g in quantise_at:
+                quantise_hidden(quantise_at[g])
+            mat_product(g)
+            z_step(g)
+            mat1_pass(g + 1)
+            bias1_pass(g + 1)
+            mat2_pass(g + 1)
             if t >= 1:
-                gate_products(t - 1)
-            for l in range(LS):
-                network_products(t, l)
-            denominator_terms(t)
-            if not odd and t >= 2:
-                inverse_denominator(t - 2)
-                inverse_denominator(t - 1)
-            if t + 1 < ROUNDS:
-                for r in range(BLOCKS):
-                    hidden_block(t + 1, r)
-            if odd:
-                gates(t)
-            network_exp(t, 0)
-            network_exp(t, 1)
-            if t >= 2:
-                finish_ratio(t - 2)
-            network_exp(t, 2)
-            if t >= 2:
-                finish_gate(t - 2)
-                finish_base(t - 2)
-            if not odd:
-                gates(t)
-            if t + 2 < ROUNDS:
-                turn(t + 2)
-            if t + 1 < ROUNDS:
-                quantise_hidden(t + 1)
-            if t >= 2:
-                finish_store(t - 2)
-            for l in range(LS):
-                network_elu(t, l)
-            for l in range(LS):
-                numerator_term(t, l)
-            if odd:
+                (bias2_pass, eps_pass, alpha_pass)[l](t - 1)
+            if g == SLOTS - LS - 1:
+                bias2_pass(t)
+                eps_pass(t)
+            if l == 0 and t >= 2:
+                gate_step(t - 2)
+            if l == 1 and t >= 2:
+                x_scaled_step(t - 2)
+            if l == 2 and t >= 1:
+                sigmoid_step(t - 1)
+            exp_step(g)
+            following = finish_of(g + 1)
+            if following is not None and following[0] == 0:
+                inverse_denominator(following[1])
+            x_product(g + 1)
+            now = finish_of(g)
+            if now is not None:
+                finish(*now)
+            if g >= 1:
+                elu_step(g - 1)
+            if g >= 2:
+                term_step(g - 2)
+            if g == 0:
+                group_chunk(8)
+                quantise_chunks(8)
+            if g in turns:
+                turn(turns[g], (0, 1))
+            for block in blocks.get(g, ()):
+                hidden_block(*block)
+            if l == 2 and t % 2 == 1:
                 log_denominator(t - 1)
                 log_denominator(t)
-        gate_products(ROUNDS - 1)
-        inverse_denominator(ROUNDS - 2)
-        inverse_denominator(ROUNDS - 1)
-        for step in (finish_ratio, finish_gate, finish_base, finish_store):
-            step(ROUNDS - 2)
-            step(ROUNDS - 1)
+            if following is not None:
+                finish_sum(following[0], following[1], sum_bank)
+
+        n = SLOTS - LS
+        t = ROUNDS - 1
+        mat_product(n)
+        z_step(n)
+        mat1_pass(n + 1)
+        mat2_pass(n + 1)
+        mat1_pass(n + 2)
+        mat2_pass(n + 2)
+        bias1_pass(n + 1)
+        alpha_pass(t - 1)
+        bias2_pass(t)
+        exp_step(n)
+        gate_step(t - 2)
+        x_product(n + 1)
+        finish(2, 4)
+        mat_product(n + 1)
+        elu_step(n - 1)
+        term_step(n - 2)
+        x_product(n + 2)
+        mat_product(n + 2)
+        eps_pass(t)
+        alpha_pass(t)
+        bias1_pass(n + 2)
+        x_scaled_step(t - 2)
+        finish_sum(0, 5, sum_bank)
+        inverse_denominator(5)
+        sigmoid_step(t - 1)
+        gate_step(t - 1)
+        x_scaled_step(t - 1)
+        log_denominator(t - 1)
+        log_denominator(t)
+        z_step(n + 1)
+        finish(0, 5)
+        finish_sum(1, 5, sum_bank)
+        z_step(n + 2)
+        term_step(n - 1)
+        finish(1, 5)
+        finish_sum(2, 5, sum_bank)
+        elu_step(n)
+        exp_step(n + 1)
+        exp_step(n + 2)
+        sigmoid_step(t)
+        gate_step(t)
+        x_scaled_step(t)
+        inverse_denominator(t - 1)
+        inverse_denominator(t)
+        finish(2, 5)
+        term_step(n)
+        finish_sum(0, t - 1, sum_bank)
+        finish_sum(1, t - 1, vector_bank)
+        finish_sum(2, t - 1, vector_bank)
+        elu_step(n + 1)
+        elu_step(n + 2)
+        finish(0, t - 1)
+        term_step(n + 1)
+        term_step(n + 2)
+        finish_sum(0, t, sum_bank)
+        finish_sum(1, t, vector_bank)
+        finish_sum(2, t, vector_bank)
+        finish(1, t - 1)
+        finish(2, t - 1)
+        for step in range(LS):
+            finish(step, t)

@@ -401,17 +401,22 @@ def tile_cn_pa_t_kernel(tc, x, cond, W1, b1, W2, b2, out):
             t, step = divmod(g - first_finish, LS)
             return step, t
 
+        mat1_early = {0: (1,), 2: (3,)}
+        mat1_late = {1: ()}
         for g in range(SLOTS - LS):
             t, l = divmod(g, LS)
             if g in quantise_at:
                 quantise_hidden(quantise_at[g])
             mat_product(g)
             z_step(g)
-            mat1_pass(g + 1)
+            for ahead in mat1_early.get(g, ()):
+                mat1_pass(ahead)
             bias1_pass(g + 1)
             mat2_pass(g + 1)
             if t >= 1:
                 (bias2_pass, eps_pass, alpha_pass)[l](t - 1)
+            for ahead in mat1_late.get(g, (g + 2,)):
+                mat1_pass(ahead)
             if g == SLOTS - LS - 1:
                 bias2_pass(t)
                 eps_pass(t)
@@ -450,7 +455,6 @@ def tile_cn_pa_t_kernel(tc, x, cond, W1, b1, W2, b2, out):
         t = ROUNDS - 1
         mat_product(n)
         z_step(n)
-        mat1_pass(n + 1)
         mat2_pass(n + 1)
         mat1_pass(n + 2)
         mat2_pass(n + 2)

@@ -69,6 +69,8 @@ def tile_cn_pa_t_kernel(tc, x, cond, W1, b1, W2, b2, out):
             which[t] = rows.tile([P, BLOCKS, DIM], BF16, name=name)
             nc.sync.dma_start(out=which[t][:], in_=source[:, t * BLOCKS : (t + 1) * BLOCKS, :])
 
+        ones_f = consts.tile([P, P], F32)
+        nc.vector.memset(ones_f[:], 1.0)
         w1_sb = consts.tile([P, HID], BF16)
         nc.sync.dma_start(out=w1_sb[:], in_=W1)
         b1_row = consts.tile([P, HID], BF16)
@@ -94,6 +96,9 @@ def tile_cn_pa_t_kernel(tc, x, cond, W1, b1, W2, b2, out):
         for t in range(2, ROUNDS):
             load_rows(t, cond_t, "cond_t", cond_rows)
             load_rows(t, x_t, "x_t", x_rows)
+        b1_all = consts.tile([P, HID], BF16)
+        nc.sync.dma_start(out=b1_all[:], in_=b1.partition_broadcast(P))
+        b1_rows = consts.tile([P, PACK, P], F32)
 
         ident_bf = consts.tile([P, P], BF16)
         make_identity(nc, ident_bf[:])
@@ -107,6 +112,11 @@ def tile_cn_pa_t_kernel(tc, x, cond, W1, b1, W2, b2, out):
         nc.vector.memset(ones[:], 1.0)
         w1_r = consts.tile([P, PACK, P], BF16)
         nc.vector.tensor_copy(out=w1_r[:], in_=w1_sb[:].rearrange("d (p j) -> d j p", j=PACK))
+
+        def warm_up(count):
+            idle = sum_bank([P, P], F32)
+            for i in range(count):
+                nc.tensor.matmul(out=idle[:], lhsT=ones_f[:], rhs=ones_f[:], start=True, stop=True)
 
         turned = {}
         grouped = {}
@@ -124,7 +134,11 @@ def tile_cn_pa_t_kernel(tc, x, cond, W1, b1, W2, b2, out):
             part_range = slice(parts[0], parts[-1] + 1)
             nc.scalar.copy(out=turned[t][:, part_range, :], in_=turned_ps[:, part_range, :])
 
+        warm_up(3)
         turn(0, (0,))
+        warm_up(1)
+        b1_planes = consts.tile([P, PACK, P], BF16)
+        nc.vector.tensor_copy(out=b1_planes[:], in_=b1_row[:].rearrange("o (p j) -> o j p", j=PACK))
         b2_ps = vector_bank([P, 2 * LS, P], BF16)
         for l in range(LS):
             nc.tensor.transpose(b2_ps[:, l, :], b2_row[:, l:SECTION:LS], ident_bf[:])
@@ -138,8 +152,6 @@ def tile_cn_pa_t_kernel(tc, x, cond, W1, b1, W2, b2, out):
         nc.vector.tensor_scalar_mul(out=eps_bias[:], in0=bias[:, LS + EPS, 3:4], scalar1=0.05)
         alpha_bias = consts.tile([P, 1], F32)
         nc.vector.tensor_scalar_mul(out=alpha_bias[:], in0=bias[:, LS + ALPHA, 3:4], scalar1=0.1)
-        b1_planes = consts.tile([P, PACK, P], BF16)
-        nc.vector.tensor_copy(out=b1_planes[:], in_=b1_row[:].rearrange("o (p j) -> o j p", j=PACK))
         def hidden_block(t, r):
             if r == 0:
                 grouped[t] = hidden.tile([P, COLS, PACK], BF16, name="grouped", align_bytes=64)
@@ -178,11 +190,17 @@ def tile_cn_pa_t_kernel(tc, x, cond, W1, b1, W2, b2, out):
                 out=w2_grp[:, c, :, :], in_=w2_raw[s][:].rearrange("p j (d l) -> p l d j", l=LS)[:, l, :, :]
             )
 
-        def quantise_chunks(c):
+        def quantise_chunks(first, end):
             nc.vector.quantize_mx(
-                out=w2_codes[:, c : c + 4, :].rearrange("p c d -> p (c d)").bitcast(FP8X4),
-                scales=w2_scales[:, c : c + 4, :].rearrange("p c d -> p (c d)"),
-                in_=w2_grp[:, c : c + 4, :, :].rearrange("p c d j -> p (c d j)"),
+                out=w2_codes[:, first:end, :].rearrange("p c d -> p (c d)").bitcast(FP8X4),
+                scales=w2_scales[:, first:end, :].rearrange("p c d -> p (c d)"),
+                in_=w2_grp[:, first:end, :, :].rearrange("p c d j -> p (c d j)"),
+            )
+
+        def group_last_section(part):
+            nc.gpsimd.tensor_scalar(
+                out=w2_grp[:, 9 + part, :, :], in0=w2_raw[3][:].rearrange("p j (s d) -> p s d j", s=LS)[:, part, :, :],
+                scalar1=1.0, scalar2=0.0, op0=ALU.mult, op1=ALU.add,
             )
 
         def params(t, section, part, bank):
@@ -360,31 +378,19 @@ def tile_cn_pa_t_kernel(tc, x, cond, W1, b1, W2, b2, out):
         turn(0, (1,))
         for c in range(4):
             group_chunk(c)
-        quantise_chunks(0)
-        for c in range(4, 6):
-            group_chunk(c)
+        quantise_chunks(0, 4)
         quantise_hidden(0)
-        turn(1, (0, 1))
-        hidden_block(1, 0)
         mat2_pass(0)
         mat1_pass(0)
         bias1_pass(0)
-        for part in range(LS):
-            nc.gpsimd.tensor_scalar(
-                out=w2_grp[:, 9 + part, :, :], in0=w2_raw[3][:].rearrange("p j (s d) -> p s d j", s=LS)[:, part, :, :],
-                scalar1=1.0, scalar2=0.0, op0=ALU.mult, op1=ALU.add,
-            )
-        for c in range(6, 8):
+        for c in range(4, 8):
             group_chunk(c)
         x_product(0)
-        quantise_chunks(4)
-        b1_ps = scalar_bank([P, HID], F32)
-        nc.tensor.matmul(out=b1_ps[:], lhsT=ones[:], rhs=b1_row[:], start=True, stop=True)
-        b1_rows = consts.tile([P, PACK, P], F32)
-        nc.vector.tensor_copy(out=b1_rows[:], in_=b1_ps[:].rearrange("w (p j) -> w j p", j=PACK))
-
-        turns = {1: 2, 2: 3}
-        blocks = {0: [(1, 1), (1, 2)], 1: [(1, 3)], 2: [(2, 0), (2, 1), (2, 2)], 3: [(2, 3), (3, 0)], 4: [(3, 1), (3, 2)], 5: [(3, 3)]}
+        quantise_chunks(4, 8)
+        turn(1, (0, 1))
+        hidden_block(1, 0)
+        turns = {0: 2, 2: 3}
+        blocks = {0: [(1, 1), (1, 2), (1, 3)], 1: [(2, 0), (2, 1)], 2: [(2, 2), (2, 3)], 3: [(3, 0), (3, 1)], 4: [(3, 2), (3, 3)]}
         for t in range(4, ROUNDS):
             turns[LS * (t - 2) - 1] = t
             for l in (0, 1):
@@ -420,16 +426,26 @@ def tile_cn_pa_t_kernel(tc, x, cond, W1, b1, W2, b2, out):
             if g == SLOTS - LS - 1:
                 bias2_pass(t)
                 eps_pass(t)
+            if g == 0:
+                group_last_section(0)
+                group_last_section(1)
+            if g == 1:
+                group_last_section(2)
+            if g == 4:
+                nc.gpsimd.tensor_scalar(
+                    out=b1_rows[:], in0=b1_all[:].rearrange("w (p j) -> w j p", j=PACK),
+                    scalar1=1.0, scalar2=0.0, op0=ALU.mult, op1=ALU.add,
+                )
             if l == 0 and t >= 2:
                 gate_step(t - 2)
             if l == 1 and t >= 2:
                 x_scaled_step(t - 2)
             if l == 2 and t >= 1:
                 sigmoid_step(t - 1)
-            exp_step(g)
             following = finish_of(g + 1)
             if following is not None and following[0] == 0:
                 inverse_denominator(following[1])
+            exp_step(g)
             x_product(g + 1)
             now = finish_of(g)
             if now is not None:
@@ -440,7 +456,10 @@ def tile_cn_pa_t_kernel(tc, x, cond, W1, b1, W2, b2, out):
                 term_step(g - 2)
             if g == 0:
                 group_chunk(8)
-                quantise_chunks(8)
+                quantise_chunks(8, 9)
+            if g == 2:
+                quantise_chunks(9, 11)
+                quantise_chunks(11, 12)
             if g in turns:
                 turn(turns[g], (0, 1))
             for block in blocks.get(g, ()):

@@ -407,6 +407,13 @@ def tile_cn_pa_t_kernel(tc, x, cond, W1, b1, W2, b2, out):
             t, step = divmod(g - first_finish, LS)
             return step, t
 
+        passes = [[] for g in range(SLOTS)]
+        products = [[] for g in range(SLOTS)]
+        for t in range(ROUNDS):
+            for l, step in enumerate((bias2_pass, eps_pass, alpha_pass)):
+                passes[LS * (t + 1) + l if t < 5 else 13 + t].append((step, t))
+            for l, step in enumerate((sigmoid_step, gate_step, x_scaled_step)):
+                products[LS * (t + 1) + 2 + l if t < 5 else (19, 20, 20, 21, 21, 22, 22, 23, 23)[LS * (t - 5) + l]].append((step, t))
         mat1_early = {0: (1,), 2: (3,)}
         mat1_late = {1: ()}
         for g in range(SLOTS - LS):
@@ -419,13 +426,14 @@ def tile_cn_pa_t_kernel(tc, x, cond, W1, b1, W2, b2, out):
                 mat1_pass(ahead)
             bias1_pass(g + 1)
             mat2_pass(g + 1)
-            if t >= 1:
-                (bias2_pass, eps_pass, alpha_pass)[l](t - 1)
+            if g < 18:
+                for step, r in passes[g]:
+                    step(r)
             for ahead in mat1_late.get(g, (g + 2,)):
                 mat1_pass(ahead)
             if g == SLOTS - LS - 1:
-                bias2_pass(t)
-                eps_pass(t)
+                mat1_pass(g + 3)
+                mat2_pass(g + 2)
             if g == 0:
                 group_last_section(0)
                 group_last_section(1)
@@ -436,16 +444,15 @@ def tile_cn_pa_t_kernel(tc, x, cond, W1, b1, W2, b2, out):
                     out=b1_rows[:], in0=b1_all[:].rearrange("w (p j) -> w j p", j=PACK),
                     scalar1=1.0, scalar2=0.0, op0=ALU.mult, op1=ALU.add,
                 )
-            if l == 0 and t >= 2:
-                gate_step(t - 2)
-            if l == 1 and t >= 2:
-                x_scaled_step(t - 2)
-            if l == 2 and t >= 1:
-                sigmoid_step(t - 1)
+            for step, r in products[g]:
+                step(r)
             following = finish_of(g + 1)
             if following is not None and following[0] == 0:
                 inverse_denominator(following[1])
             exp_step(g)
+            if g >= 18:
+                for step, r in passes[g]:
+                    step(r)
             x_product(g + 1)
             now = finish_of(g)
             if now is not None:
@@ -474,61 +481,51 @@ def tile_cn_pa_t_kernel(tc, x, cond, W1, b1, W2, b2, out):
         t = ROUNDS - 1
         mat_product(n)
         z_step(n)
-        mat2_pass(n + 1)
-        mat1_pass(n + 2)
         mat2_pass(n + 2)
         bias1_pass(n + 1)
-        alpha_pass(t - 1)
-        bias2_pass(t)
+        bias1_pass(n + 2)
         exp_step(n)
-        gate_step(t - 2)
+        for step, r in products[n]:
+            step(r)
         x_product(n + 1)
-        finish(2, 4)
         mat_product(n + 1)
+        finish(2, 4)
+        mat_product(n + 2)
+        x_product(n + 2)
         elu_step(n - 1)
         term_step(n - 2)
-        x_product(n + 2)
-        mat_product(n + 2)
-        eps_pass(t)
-        alpha_pass(t)
-        bias1_pass(n + 2)
-        x_scaled_step(t - 2)
-        finish_sum(0, 5, sum_bank)
+        for step, r in products[n + 1] + products[n + 2]:
+            step(r)
         inverse_denominator(5)
-        sigmoid_step(t - 1)
-        gate_step(t - 1)
-        x_scaled_step(t - 1)
         log_denominator(t - 1)
+        finish_sum(0, 5, sum_bank)
         log_denominator(t)
+        finish_sum(1, 5, vector_bank)
+        finish_sum(2, 5, vector_bank)
         z_step(n + 1)
-        finish(0, 5)
-        finish_sum(1, 5, sum_bank)
         z_step(n + 2)
+        finish(0, 5)
         term_step(n - 1)
         finish(1, 5)
-        finish_sum(2, 5, sum_bank)
         elu_step(n)
-        exp_step(n + 1)
-        exp_step(n + 2)
-        sigmoid_step(t)
-        gate_step(t)
-        x_scaled_step(t)
-        inverse_denominator(t - 1)
-        inverse_denominator(t)
         finish(2, 5)
-        term_step(n)
         finish_sum(0, t - 1, sum_bank)
         finish_sum(1, t - 1, vector_bank)
         finish_sum(2, t - 1, vector_bank)
+        exp_step(n + 1)
+        exp_step(n + 2)
+        inverse_denominator(t - 1)
+        inverse_denominator(t)
+        term_step(n)
         elu_step(n + 1)
         elu_step(n + 2)
         finish(0, t - 1)
         term_step(n + 1)
+        finish(1, t - 1)
         term_step(n + 2)
-        finish_sum(0, t, sum_bank)
         finish_sum(1, t, vector_bank)
         finish_sum(2, t, vector_bank)
-        finish(1, t - 1)
+        finish_sum(0, t, sum_bank)
         finish(2, t - 1)
         for step in range(LS):
             finish(step, t)

@@ -27,6 +27,8 @@ SECTION = LS * DIM
 MAT1, BIAS1, MAT2 = 0, 1, 2
 BIAS2, EPS, ALPHA = 0, 1, 2
 MATMUL_BIAS_ROUNDS = 5
+NT = 14
+FIN = tuple((g, 1) for g in range(10, 21))
 LOWEST = -3.0e38
 CHUNKS = (
     (MAT2, 0), (MAT1, 0), (BIAS1, 0), (MAT2, 1),
@@ -278,7 +280,7 @@ def tile_cn_pa_t_kernel(tc, x, cond, W1, b1, W2, b2, out):
 
         def mat_product(g):
             t, l = divmod(g, LS)
-            den_term[g] = kept.tile([P, COLS], F32, name="den_term", bufs=9)
+            den_term[g] = kept.tile([P, COLS], F32, name="den_term", bufs=12)
             nc.vector.scalar_tensor_tensor(
                 out=den_term[g][:], in0=mat1_ps[g][:], scalar=bias[:, l, MAT1 : MAT1 + 1], in1=mat2[g][:],
                 op0=ALU.add, op1=ALU.mult,
@@ -302,20 +304,20 @@ def tile_cn_pa_t_kernel(tc, x, cond, W1, b1, W2, b2, out):
             )
 
         def elu_step(g):
-            elu_plus_one[g] = work.tile([P, COLS], F32, name="elu_plus_one")
+            elu_plus_one[g] = kept.tile([P, COLS], F32, name="num_term", bufs=NT)
             nc.vector.scalar_tensor_tensor(
                 out=elu_plus_one[g][:], in0=exp_z[g][:], scalar=1.0, in1=z_plus_one[g][:], op0=ALU.min, op1=ALU.max,
             )
 
         def term_step(g):
-            num_term[g] = kept.tile([P, COLS], F32, name="num_term", bufs=9)
+            num_term[g] = elu_plus_one[g]
             nc.vector.scalar_tensor_tensor(
                 out=num_term[g][:], in0=elu_plus_one[g][:], scalar=-1.0, in1=mat2[g][:], op0=ALU.add, op1=ALU.mult,
             )
 
         def bias2_pass(t):
             ps = params(t, 3, BIAS2, scalar_bank)
-            bias2[t] = kept.tile([P, COLS], F32, name="bias2", bufs=4)
+            bias2[t] = kept.tile([P, COLS], F32, name="bias2", bufs=5)
             nc.scalar.activation(
                 out=bias2[t][:], in_=ps[:], func=ACT.Identity, bias=bias[:, LS + BIAS2, 3:4], scale=1.0
             )
@@ -337,16 +339,16 @@ def tile_cn_pa_t_kernel(tc, x, cond, W1, b1, W2, b2, out):
             )
 
         def gate_step(t):
-            gate[t] = kept.tile([P, COLS], F32, name="gate", bufs=3)
+            gate[t] = kept.tile([P, COLS], F32, name="gate", bufs=5)
             nc.gpsimd.tensor_tensor(out=gate[t][:], in0=sigmoid_eps[t][:], in1=exp_alpha[t][:], op=ALU.mult)
 
         def x_scaled_step(t):
-            x_scaled[t] = kept.tile([P, COLS], F32, name="x_scaled", bufs=3)
+            x_scaled[t] = kept.tile([P, COLS], F32, name="x_scaled", bufs=5)
             nc.gpsimd.tensor_tensor(out=x_scaled[t][:], in0=exp_alpha[t][:], in1=turned[t][:, 1, :], op=ALU.mult)
 
         def log_denominator(t):
             den_ps = transposed_sum([den_term[LS * t + l] for l in range(LS)], scalar_bank)
-            log_den[t] = last.tile([P, COLS], F32, name="log_den")
+            log_den[t] = last.tile([P, COLS], F32, name="log_den", bufs=3)
             nc.scalar.activation(out=log_den[t][:], in_=den_ps, func=ACT.Ln, bias=plus_one[:], scale=-1.0)
 
         def inverse_denominator(t):
@@ -399,19 +401,17 @@ def tile_cn_pa_t_kernel(tc, x, cond, W1, b1, W2, b2, out):
         for t in range(2, ROUNDS):
             quantise_at[LS * (t - 1) + 1] = t
 
-        first_finish = 7
-
-        def finish_of(g):
-            if g < first_finish:
-                return None
-            t, step = divmod(g - first_finish, LS)
-            return step, t
+        logs_at = {8: (0, 1, 2), 17: (3, 4, 5)}
+        steps = [(step, t) for t in range(ROUNDS) for step in range(LS)]
+        finishes = {}
+        for g, count in FIN:
+            finishes[g] = [steps.pop(0) for i in range(count)]
 
         passes = [[] for g in range(SLOTS)]
         products = [[] for g in range(SLOTS)]
         for t in range(ROUNDS):
             for l, step in enumerate((bias2_pass, eps_pass, alpha_pass)):
-                passes[LS * (t + 1) + l if t < 5 else 13 + t].append((step, t))
+                passes[LS * (t + 1) + l if t < 5 else (18, 18, 19, 19, 20, 20, 21, 21, 21)[LS * (t - 5) + l]].append((step, t))
             for l, step in enumerate((sigmoid_step, gate_step, x_scaled_step)):
                 products[LS * (t + 1) + 2 + l if t < 5 else (19, 20, 20, 21, 21, 22, 22, 23, 23)[LS * (t - 5) + l]].append((step, t))
         mat1_early = {0: (1,), 2: (3,)}
@@ -446,21 +446,26 @@ def tile_cn_pa_t_kernel(tc, x, cond, W1, b1, W2, b2, out):
                 )
             for step, r in products[g]:
                 step(r)
-            following = finish_of(g + 1)
-            if following is not None and following[0] == 0:
-                inverse_denominator(following[1])
+            following = finishes.get(g + 1, ())
+            for step, r in following:
+                if step == 0:
+                    inverse_denominator(r)
             exp_step(g)
             if g >= 18:
                 for step, r in passes[g]:
                     step(r)
             x_product(g + 1)
-            now = finish_of(g)
-            if now is not None:
-                finish(*now)
+            now = finishes.get(g, ())
+            if len(now) > 0:
+                finish(*now[0])
+            if len(now) > 1:
+                finish_sum(*now[1], sum_bank)
             if g >= 1:
                 elu_step(g - 1)
             if g >= 2:
                 term_step(g - 2)
+            if len(now) > 1:
+                finish(*now[1])
             if g == 0:
                 group_chunk(8)
                 quantise_chunks(8, 9)
@@ -471,61 +476,81 @@ def tile_cn_pa_t_kernel(tc, x, cond, W1, b1, W2, b2, out):
                 turn(turns[g], (0, 1))
             for block in blocks.get(g, ()):
                 hidden_block(*block)
-            if l == 2 and t % 2 == 1:
-                log_denominator(t - 1)
-                log_denominator(t)
-            if following is not None:
-                finish_sum(following[0], following[1], sum_bank)
+            for r in logs_at.get(g, ()):
+                log_denominator(r)
+            if g == SLOTS - LS - 1:
+                finish_sum(*steps[0], sum_bank)
+            if len(following) > 0:
+                finish_sum(*following[0], sum_bank)
 
         n = SLOTS - LS
         t = ROUNDS - 1
+        summed = steps[1:]
+
+        def sum_next(bank):
+            step = summed.pop(0)
+            finish_sum(*step, bank)
+
+        def finish_next():
+            step = steps.pop(0)
+            finish(*step)
+
         mat_product(n)
         z_step(n)
         mat2_pass(n + 2)
         bias1_pass(n + 1)
-        bias1_pass(n + 2)
+        inverse_denominator(4)
         exp_step(n)
+        for step, r in passes[n]:
+            step(r)
+        inverse_denominator(5)
+        bias1_pass(n + 2)
         for step, r in products[n]:
             step(r)
         x_product(n + 1)
         mat_product(n + 1)
-        finish(2, 4)
+        finish_next()
+        sum_next(sum_bank)
         mat_product(n + 2)
         x_product(n + 2)
-        elu_step(n - 1)
-        term_step(n - 2)
         for step, r in products[n + 1] + products[n + 2]:
             step(r)
-        inverse_denominator(5)
+        elu_step(n - 1)
+        term_step(n - 2)
         log_denominator(t - 1)
-        finish_sum(0, 5, sum_bank)
         log_denominator(t)
-        finish_sum(1, 5, vector_bank)
-        finish_sum(2, 5, vector_bank)
+        sum_next(vector_bank)
+        sum_next(vector_bank)
         z_step(n + 1)
         z_step(n + 2)
-        finish(0, 5)
+        sum_next(vector_bank)
+        sum_next(vector_bank)
+        finish_next()
+        sum_next(sum_bank)
         term_step(n - 1)
-        finish(1, 5)
+        finish_next()
+        sum_next(vector_bank)
         elu_step(n)
-        finish(2, 5)
-        finish_sum(0, t - 1, sum_bank)
-        finish_sum(1, t - 1, vector_bank)
-        finish_sum(2, t - 1, vector_bank)
+        finish_next()
+        sum_next(vector_bank)
+        finish_next()
+        sum_next(vector_bank)
+        term_step(n)
+        finish_next()
+        finish_next()
         exp_step(n + 1)
         exp_step(n + 2)
         inverse_denominator(t - 1)
         inverse_denominator(t)
-        term_step(n)
         elu_step(n + 1)
         elu_step(n + 2)
-        finish(0, t - 1)
+        finish_next()
         term_step(n + 1)
-        finish(1, t - 1)
+        finish_next()
         term_step(n + 2)
         finish_sum(1, t, vector_bank)
         finish_sum(2, t, vector_bank)
         finish_sum(0, t, sum_bank)
-        finish(2, t - 1)
-        for step in range(LS):
-            finish(step, t)
+        finish_next()
+        for i in range(LS):
+            finish_next()

@@ -148,12 +148,6 @@ def tile_cn_pa_t_kernel(tc, x, cond, W1, b1, W2, b2, out):
             nc.tensor.transpose(b2_ps[:, LS + part, :], b2_row[:, part * P : (part + 1) * P], ident_bf[:])
         bias = consts.tile([P, 2 * LS, 4], F32)
         nc.vector.tensor_copy(out=bias[:], in_=b2_ps[:, :, 0:4])
-        bias1_plus_one = consts.tile([P, LS], F32)
-        nc.vector.tensor_scalar_add(out=bias1_plus_one[:], in0=bias[:, 0:LS, BIAS1], scalar1=1.0)
-        eps_bias = consts.tile([P, 1], F32)
-        nc.vector.tensor_scalar_mul(out=eps_bias[:], in0=bias[:, LS + EPS, 3:4], scalar1=0.05)
-        alpha_bias = consts.tile([P, 1], F32)
-        nc.vector.tensor_scalar_mul(out=alpha_bias[:], in0=bias[:, LS + ALPHA, 3:4], scalar1=0.1)
         def hidden_block(t, r):
             if r == 0:
                 grouped[t] = hidden.tile([P, COLS, PACK], BF16, name="grouped", align_bytes=64)
@@ -219,9 +213,9 @@ def tile_cn_pa_t_kernel(tc, x, cond, W1, b1, W2, b2, out):
             )
             return p_ps
 
-        def transposed_sum(terms, bank):
+        def transposed_sum(terms, bank, blocks=range(BLOCKS)):
             total = bank([P, BLOCKS, P], F32)
-            for r in range(BLOCKS):
+            for r in blocks:
                 for i, term in enumerate(terms):
                     nc.tensor.matmul(
                         out=total[:, r, :],
@@ -231,7 +225,7 @@ def tile_cn_pa_t_kernel(tc, x, cond, W1, b1, W2, b2, out):
                         start=(i == 0),
                         stop=(i == len(terms) - 1),
                     )
-            return total[:].rearrange("p r d -> p (r d)")
+            return total[:].rearrange("p r d -> p (r d)")[:, blocks[0] * P : (blocks[-1] + 1) * P]
 
         mat2 = {}
         mat1_ps = {}
@@ -378,21 +372,31 @@ def tile_cn_pa_t_kernel(tc, x, cond, W1, b1, W2, b2, out):
         for r in range(BLOCKS):
             hidden_block(0, r)
         turn(0, (1,))
-        for c in range(4):
+        group_chunk(0)
+        group_chunk(1)
+        bias1_plus_one = consts.tile([P, LS], F32)
+        nc.vector.tensor_scalar_add(out=bias1_plus_one[:], in0=bias[:, 0:LS, BIAS1], scalar1=1.0)
+        eps_bias = consts.tile([P, 1], F32)
+        nc.vector.tensor_scalar_mul(out=eps_bias[:], in0=bias[:, LS + EPS, 3:4], scalar1=0.05)
+        alpha_bias = consts.tile([P, 1], F32)
+        nc.vector.tensor_scalar_mul(out=alpha_bias[:], in0=bias[:, LS + ALPHA, 3:4], scalar1=0.1)
+        for c in range(2, 5):
             group_chunk(c)
         quantise_chunks(0, 4)
-        quantise_hidden(0)
-        mat2_pass(0)
-        mat1_pass(0)
-        bias1_pass(0)
-        for c in range(4, 8):
-            group_chunk(c)
-        x_product(0)
-        quantise_chunks(4, 8)
         turn(1, (0, 1))
+        quantise_hidden(0)
+        mat1_pass(0)
+        mat2_pass(0)
+        bias1_pass(0)
+        for c in range(5, 9):
+            group_chunk(c)
+        quantise_chunks(4, 8)
+        x_product(0)
         hidden_block(1, 0)
+        hidden_block(1, 1)
+
         turns = {0: 2, 2: 3}
-        blocks = {0: [(1, 1), (1, 2), (1, 3)], 1: [(2, 0), (2, 1)], 2: [(2, 2), (2, 3)], 3: [(3, 0), (3, 1)], 4: [(3, 2), (3, 3)]}
+        blocks = {0: [(1, 2), (1, 3)], 1: [(2, 0), (2, 1)], 2: [(2, 2), (2, 3)], 3: [(3, 0), (3, 1)], 4: [(3, 2), (3, 3)]}
         for t in range(4, ROUNDS):
             turns[LS * (t - 2) - 1] = t
             for l in (0, 1):
@@ -467,7 +471,6 @@ def tile_cn_pa_t_kernel(tc, x, cond, W1, b1, W2, b2, out):
             if len(now) > 1:
                 finish(*now[1])
             if g == 0:
-                group_chunk(8)
                 quantise_chunks(8, 9)
             if g == 2:
                 quantise_chunks(9, 11)
@@ -550,7 +553,23 @@ def tile_cn_pa_t_kernel(tc, x, cond, W1, b1, W2, b2, out):
         term_step(n + 2)
         finish_sum(1, t, vector_bank)
         finish_sum(2, t, vector_bank)
-        finish_sum(0, t, sum_bank)
+        halves = (range(0, 2), range(2, BLOCKS))
+        last_sums = [transposed_sum([num_term[LS * t + l] for l in range(LS)], bank, half) for bank, half in ((sum_bank, halves[0]), (vector_bank, halves[1]))]
         finish_next()
-        for i in range(LS):
-            finish_next()
+        ratio[t] = last.tile([P, COLS], F32, name="ratio")
+        moved[t] = last.tile([P, COLS], F32, name="moved")
+        result = last.tile([P, BLOCKS, DIM], F32, name="result")
+        flat = result[:].rearrange("p r d -> p (r d)")
+        for half in range(2):
+            cols = slice(half * 2 * P, (half + 1) * 2 * P)
+            nc.vector.tensor_tensor(out=ratio[t][:, cols], in0=last_sums[half], in1=inv_den[t][:, cols], op=ALU.mult)
+        for half in range(2):
+            cols = slice(half * 2 * P, (half + 1) * 2 * P)
+            nc.vector.tensor_tensor(out=moved[t][:, cols], in0=sums[1, t][:, cols], in1=ratio[t][:, cols], op=ALU.mult)
+        for half in range(2):
+            cols = slice(half * 2 * P, (half + 1) * 2 * P)
+            nc.vector.tensor_tensor(out=flat[:, cols], in0=sums[2, t][:, cols], in1=moved[t][:, cols], op=ALU.add)
+            nc.sync.dma_start(
+                out=out_rows[:, t * BLOCKS + 2 * half : t * BLOCKS + 2 * half + 2, :],
+                in_=result[:, 2 * half : 2 * half + 2, :],
+            )

@@ -27,7 +27,9 @@ SECTION = LS * DIM
 MAT1, BIAS1, MAT2 = 0, 1, 2
 BIAS2, EPS, ALPHA = 0, 1, 2
 MATMUL_BIAS_ROUNDS = 5
-NT = 14
+NT = 8
+NG = 6
+EXP2 = False
 FIN = tuple((g, 1) for g in range(10, 21))
 LOWEST = -3.0e38
 CHUNKS = (
@@ -251,9 +253,10 @@ def tile_cn_pa_t_kernel(tc, x, cond, W1, b1, W2, b2, out):
         def mat2_pass(g):
             t, l = divmod(g, LS)
             mat2_ps = params(t, MAT2, l, scalar_bank)
-            mat2[g] = work.tile([P, COLS], F32, name="mat2", bufs=5)
+            if g % 2 == 0:
+                mat2[g // 2] = work.tile([P, 2, COLS], F32, name="mat2", bufs=4)
             nc.scalar.activation(
-                out=mat2[g][:], in_=mat2_ps[:], func=ACT.Identity, bias=bias[:, l, MAT2 : MAT2 + 1], scale=1.0
+                out=mat2[g // 2][:, g % 2, :], in_=mat2_ps[:], func=ACT.Identity, bias=bias[:, l, MAT2 : MAT2 + 1], scale=1.0
             )
 
         def mat1_pass(g):
@@ -266,18 +269,19 @@ def tile_cn_pa_t_kernel(tc, x, cond, W1, b1, W2, b2, out):
 
         def x_product(g):
             t, l = divmod(g, LS)
-            x_mat1[g] = work.tile([P, COLS], F32, name="x_mat1")
+            if g % 2 == 0:
+                z_plus_one[g // 2] = work.tile([P, 2, COLS], F32, name="z_plus_one", bufs=3)
             nc.vector.scalar_tensor_tensor(
-                out=x_mat1[g][:], in0=mat1_ps[g][:], scalar=bias[:, l, MAT1 : MAT1 + 1], in1=turned[t][:, 1, :],
-                op0=ALU.add, op1=ALU.mult,
+                out=z_plus_one[g // 2][:, g % 2, :], in0=mat1_ps[g][:], scalar=bias[:, l, MAT1 : MAT1 + 1],
+                in1=turned[t][:, 1, :], op0=ALU.add, op1=ALU.mult,
             )
 
         def mat_product(g):
             t, l = divmod(g, LS)
             den_term[g] = kept.tile([P, COLS], F32, name="den_term", bufs=12)
             nc.vector.scalar_tensor_tensor(
-                out=den_term[g][:], in0=mat1_ps[g][:], scalar=bias[:, l, MAT1 : MAT1 + 1], in1=mat2[g][:],
-                op0=ALU.add, op1=ALU.mult,
+                out=den_term[g][:], in0=mat1_ps[g][:], scalar=bias[:, l, MAT1 : MAT1 + 1],
+                in1=mat2[g // 2][:, g % 2, :], op0=ALU.add, op1=ALU.mult,
             )
             nc.gpsimd.tensor_scalar(
                 out=den_term[g][:], in0=den_term[g][:], scalar1=0.0, scalar2=LOWEST, op0=ALU.min, op1=ALU.max
@@ -285,28 +289,30 @@ def tile_cn_pa_t_kernel(tc, x, cond, W1, b1, W2, b2, out):
 
         def z_step(g):
             l = g % LS
-            z_plus_one[g] = work.tile([P, COLS], F32, name="z_plus_one")
+            z = z_plus_one[g // 2][:, g % 2, :]
             nc.vector.scalar_tensor_tensor(
-                out=z_plus_one[g][:], in0=bias1_ps[g][:], scalar=bias1_plus_one[:, l : l + 1], in1=x_mat1[g][:],
-                op0=ALU.add, op1=ALU.add,
+                out=z, in0=bias1_ps[g][:], scalar=bias1_plus_one[:, l : l + 1], in1=z, op0=ALU.add, op1=ALU.add,
             )
 
-        def exp_step(g):
-            exp_z[g] = work.tile([P, COLS], F32, name="exp_z")
+        def exp_step(pair, part):
+            if pair not in exp_z:
+                exp_z[pair] = kept.tile([P, 2, COLS], F32, name="num_term", bufs=NT)
+                for j in range(2):
+                    num_term[2 * pair + j] = exp_z[pair][:, j, :]
             nc.scalar.activation(
-                out=exp_z[g][:], in_=z_plus_one[g][:], func=ACT.Exp, bias=minus_one[:], scale=1.0
+                out=exp_z[pair][:, part, :], in_=z_plus_one[pair][:, part, :], func=ACT.Exp, bias=minus_one[:], scale=1.0
             )
 
-        def elu_step(g):
-            elu_plus_one[g] = kept.tile([P, COLS], F32, name="num_term", bufs=NT)
+        def elu_step(pair, part):
+            value = exp_z[pair][:, part, :]
             nc.vector.scalar_tensor_tensor(
-                out=elu_plus_one[g][:], in0=exp_z[g][:], scalar=1.0, in1=z_plus_one[g][:], op0=ALU.min, op1=ALU.max,
+                out=value, in0=value, scalar=1.0, in1=z_plus_one[pair][:, part, :], op0=ALU.min, op1=ALU.max,
             )
 
-        def term_step(g):
-            num_term[g] = elu_plus_one[g]
+        def term_step(pair, part):
+            value = exp_z[pair][:, part, :]
             nc.vector.scalar_tensor_tensor(
-                out=num_term[g][:], in0=elu_plus_one[g][:], scalar=-1.0, in1=mat2[g][:], op0=ALU.add, op1=ALU.mult,
+                out=value, in0=value, scalar=-1.0, in1=mat2[pair][:, part, :], op0=ALU.add, op1=ALU.mult,
             )
 
         def bias2_pass(t):
@@ -318,26 +324,26 @@ def tile_cn_pa_t_kernel(tc, x, cond, W1, b1, W2, b2, out):
 
         def eps_pass(t):
             ps = params(t, 3, EPS, scalar_bank)
-            tanh_eps[t] = kept.tile([P, COLS], F32, name="tanh_eps", bufs=3)
+            tanh_eps[t] = kept.tile([P, COLS], F32, name="gate", bufs=NG)
             nc.scalar.activation(out=tanh_eps[t][:], in_=ps[:], func=ACT.Tanh, bias=eps_bias[:], scale=0.05)
 
         def alpha_pass(t):
             ps = params(t, 3, ALPHA, scalar_bank)
-            exp_alpha[t] = kept.tile([P, COLS], F32, name="exp_alpha", bufs=4)
+            exp_alpha[t] = kept.tile([P, COLS], F32, name="x_scaled", bufs=NG)
             nc.scalar.activation(out=exp_alpha[t][:], in_=ps[:], func=ACT.Exp, bias=alpha_bias[:], scale=0.1)
 
         def sigmoid_step(t):
-            sigmoid_eps[t] = kept.tile([P, COLS], F32, name="sigmoid_eps", bufs=2)
+            sigmoid_eps[t] = tanh_eps[t]
             nc.gpsimd.tensor_scalar(
                 out=sigmoid_eps[t][:], in0=tanh_eps[t][:], scalar1=1.0, scalar2=0.4, op0=ALU.add, op1=ALU.mult
             )
 
         def gate_step(t):
-            gate[t] = kept.tile([P, COLS], F32, name="gate", bufs=5)
+            gate[t] = sigmoid_eps[t]
             nc.gpsimd.tensor_tensor(out=gate[t][:], in0=sigmoid_eps[t][:], in1=exp_alpha[t][:], op=ALU.mult)
 
         def x_scaled_step(t):
-            x_scaled[t] = kept.tile([P, COLS], F32, name="x_scaled", bufs=5)
+            x_scaled[t] = exp_alpha[t]
             nc.gpsimd.tensor_tensor(out=x_scaled[t][:], in0=exp_alpha[t][:], in1=turned[t][:, 1, :], op=ALU.mult)
 
         def log_denominator(t):
@@ -408,6 +414,9 @@ def tile_cn_pa_t_kernel(tc, x, cond, W1, b1, W2, b2, out):
         logs_at = {8: (0, 1, 2), 17: (3, 4, 5)}
         steps = [(step, t) for t in range(ROUNDS) for step in range(LS)]
         finishes = {}
+        both = slice(0, 2)
+        first = slice(0, 1)
+        second = slice(1, 2)
         for g, count in FIN:
             finishes[g] = [steps.pop(0) for i in range(count)]
 
@@ -454,7 +463,11 @@ def tile_cn_pa_t_kernel(tc, x, cond, W1, b1, W2, b2, out):
             for step, r in following:
                 if step == 0:
                     inverse_denominator(r)
-            exp_step(g)
+            if EXP2:
+                if g % 2 == 1:
+                    exp_step(g // 2, both)
+            else:
+                exp_step(g // 2, slice(g % 2, g % 2 + 1))
             if g >= 18:
                 for step, r in passes[g]:
                     step(r)
@@ -464,10 +477,11 @@ def tile_cn_pa_t_kernel(tc, x, cond, W1, b1, W2, b2, out):
                 finish(*now[0])
             if len(now) > 1:
                 finish_sum(*now[1], sum_bank)
-            if g >= 1:
-                elu_step(g - 1)
             if g >= 2:
-                term_step(g - 2)
+                if g % 2 == 0:
+                    elu_step(g // 2 - 1, both)
+                if g % 2 == 1:
+                    term_step(g // 2 - 1, both)
             if len(now) > 1:
                 finish(*now[1])
             if g == 0:
@@ -488,6 +502,7 @@ def tile_cn_pa_t_kernel(tc, x, cond, W1, b1, W2, b2, out):
 
         n = SLOTS - LS
         t = ROUNDS - 1
+        steps[1:7] = [(0, 4), (0, 5), (1, 4), (1, 5), (2, 4), (2, 5)]
         summed = steps[1:]
 
         def sum_next(bank):
@@ -503,7 +518,7 @@ def tile_cn_pa_t_kernel(tc, x, cond, W1, b1, W2, b2, out):
         mat2_pass(n + 2)
         bias1_pass(n + 1)
         inverse_denominator(4)
-        exp_step(n)
+        exp_step(n // 2, both if EXP2 else second)
         for step, r in passes[n]:
             step(r)
         inverse_denominator(5)
@@ -518,8 +533,7 @@ def tile_cn_pa_t_kernel(tc, x, cond, W1, b1, W2, b2, out):
         x_product(n + 2)
         for step, r in products[n + 1] + products[n + 2]:
             step(r)
-        elu_step(n - 1)
-        term_step(n - 2)
+        term_step(n // 2 - 1, both)
         log_denominator(t - 1)
         log_denominator(t)
         sum_next(vector_bank)
@@ -528,29 +542,28 @@ def tile_cn_pa_t_kernel(tc, x, cond, W1, b1, W2, b2, out):
         z_step(n + 2)
         sum_next(vector_bank)
         sum_next(vector_bank)
+        elu_step(n // 2, both)
         finish_next()
         sum_next(sum_bank)
-        term_step(n - 1)
-        finish_next()
-        sum_next(vector_bank)
-        elu_step(n)
+        term_step(n // 2, both)
         finish_next()
         sum_next(vector_bank)
         finish_next()
         sum_next(vector_bank)
-        term_step(n)
+        finish_next()
+        sum_next(vector_bank)
         finish_next()
         finish_next()
-        exp_step(n + 1)
-        exp_step(n + 2)
+        exp_step(n // 2 + 1, first)
+        exp_step(n // 2 + 1, second)
         inverse_denominator(t - 1)
         inverse_denominator(t)
-        elu_step(n + 1)
-        elu_step(n + 2)
+        elu_step(n // 2 + 1, first)
+        elu_step(n // 2 + 1, second)
         finish_next()
-        term_step(n + 1)
+        term_step(n // 2 + 1, first)
         finish_next()
-        term_step(n + 2)
+        term_step(n // 2 + 1, second)
         finish_sum(1, t, vector_bank)
         finish_sum(2, t, vector_bank)
         halves = (range(0, 2), range(2, BLOCKS))

from contextlib import ExitStack

import concourse.mybir as mybir
from concourse.masks import make_identity

F32 = mybir.dt.float32
BF16 = mybir.dt.bfloat16
U32 = mybir.dt.uint32
U8 = mybir.dt.uint8
FP8X4 = mybir.dt.float8_e4m3fn_x4
ACT = mybir.ActivationFunctionType
ALU = mybir.AluOpType

P = 128
PACK = 4
BATCH = 4096
DIM = 128
HID = 512
LS = 3
PARAMS = 1536
COLS = 512
BLOCKS = COLS // P
ROUNDS = BATCH // COLS
SLOTS = ROUNDS * LS
ROWS_PER_PARTITION = BATCH // P
SECTION = LS * DIM
MAT1, BIAS1, MAT2 = 0, 1, 2
BIAS2, EPS, ALPHA = 0, 1, 2
MATMUL_BIAS_ROUNDS = 5
NT = 8
NG = 6
EXP2 = False
FIN = tuple((g, 1) for g in range(10, 21))
LOWEST = -3.0e38
CHUNKS = (
    (MAT2, 0), (MAT1, 0), (BIAS1, 0), (MAT2, 1),
    (MAT1, 1), (BIAS1, 1), (MAT2, 2), (MAT1, 2),
    (BIAS1, 2), (3, BIAS2), (3, EPS), (3, ALPHA),
)

FLOPS = 2 * BATCH * DIM * HID + 2 * BATCH * HID * PARAMS


def tile_cn_pa_t_kernel(tc, x, cond, W1, b1, W2, b2, out):
    nc = tc.nc
    x_rows = x.rearrange("(p r) d -> p r d", r=ROWS_PER_PARTITION)
    cond_rows = cond.rearrange("(p r) d -> p r d", r=ROWS_PER_PARTITION)
    out_rows = out.rearrange("(p r) d -> p r d", r=ROWS_PER_PARTITION)

    with ExitStack() as ctx:
        ctx.enter_context(tc.manual_schedule())
        consts = ctx.enter_context(tc.tile_pool(name="consts", bufs=1))
        rows = ctx.enter_context(tc.tile_pool(name="rows", bufs=ROUNDS))
        hidden = ctx.enter_context(tc.tile_pool(name="hidden", bufs=3))
        work = ctx.enter_context(tc.tile_pool(name="work", bufs=3))
        kept = ctx.enter_context(tc.tile_pool(name="kept", bufs=3))
        last = ctx.enter_context(tc.tile_pool(name="last", bufs=2))
        psum = ctx.enter_context(tc.psum_pool(name="psum", bufs=1))

        def vector_bank(shape, dtype):
            return psum.tile(shape, dtype, name="vector_bank", tag="vector_bank", bufs=4)

        def scalar_bank(shape, dtype):
            return psum.tile(shape, dtype, name="scalar_bank", tag="scalar_bank", bufs=3)

        def sum_bank(shape, dtype):
            return psum.tile(shape, dtype, name="sum_bank", tag="sum_bank", bufs=1)

        cond_t = {}
        x_t = {}

        def load_rows(t, which, name, source):
            which[t] = rows.tile([P, BLOCKS, DIM], BF16, name=name)
            nc.sync.dma_start(out=which[t][:], in_=source[:, t * BLOCKS : (t + 1) * BLOCKS, :])

        ones_f = consts.tile([P, P], F32)
        nc.vector.memset(ones_f[:], 1.0)
        w1_sb = consts.tile([P, HID], BF16)
        nc.sync.dma_start(out=w1_sb[:], in_=W1)
        b1_row = consts.tile([P, HID], BF16)
        nc.vector.memset(b1_row[:], 0.0)
        b2_row = consts.tile([P, SECTION], BF16)
        nc.vector.memset(b2_row[:], 0.0)
        load_rows(0, cond_t, "cond_t", cond_rows)
        nc.sync.dma_start(out=b1_row[0:1, :], in_=b1.rearrange("(o k) -> o k", o=1))
        nc.sync.dma_start(out=b2_row[0:4, :], in_=b2.rearrange("(s c) -> s c", s=4))
        w2_rows = W2.rearrange("(p j) c -> p j c", j=PACK)
        w2_raw = {}

        def load_w2(s):
            w2_raw[s] = consts.tile([P, PACK, SECTION], BF16, name="w2_raw%d" % s)
            nc.sync.dma_start(out=w2_raw[s][:], in_=w2_rows[:, :, s * SECTION : (s + 1) * SECTION])

        for s in (MAT2, MAT1, BIAS1):
            load_w2(s)
        load_rows(0, x_t, "x_t", x_rows)
        load_rows(1, cond_t, "cond_t", cond_rows)
        load_rows(1, x_t, "x_t", x_rows)
        load_w2(3)
        for t in range(2, ROUNDS):
            load_rows(t, cond_t, "cond_t", cond_rows)
            load_rows(t, x_t, "x_t", x_rows)
        b1_all = consts.tile([P, HID], BF16)
        nc.sync.dma_start(out=b1_all[:], in_=b1.partition_broadcast(P))
        b1_rows = consts.tile([P, PACK, P], F32)

        ident_bf = consts.tile([P, P], BF16)
        make_identity(nc, ident_bf[:])
        ident_f = consts.tile([P, P], F32)
        make_identity(nc, ident_f[:])
        minus_one = consts.tile([P, 1], F32)
        nc.vector.memset(minus_one[:], -1.0)
        plus_one = consts.tile([P, 1], F32)
        nc.vector.memset(plus_one[:], 1.0)
        ones = consts.tile([P, P], BF16)
        nc.vector.memset(ones[:], 1.0)
        w1_r = consts.tile([P, PACK, P], BF16)
        nc.vector.tensor_copy(out=w1_r[:], in_=w1_sb[:].rearrange("d (p j) -> d j p", j=PACK))

        def warm_up(count):
            idle = sum_bank([P, P], F32)
            for i in range(count):
                nc.tensor.matmul(out=idle[:], lhsT=ones_f[:], rhs=ones_f[:], start=True, stop=True)

        turned = {}
        grouped = {}
        h_codes = {}
        h_scales = {}

        def turn(t, parts):
            if t not in turned:
                turned[t] = hidden.tile([P, 2, COLS], BF16, name="turned", bufs=5)
            turned_ps = scalar_bank([P, 2, COLS], BF16)
            for part in parts:
                source = (cond_t, x_t)[part][t]
                for r in range(BLOCKS):
                    nc.tensor.transpose(turned_ps[:, part, r * P : (r + 1) * P], source[:, r, :], ident_bf[:])
            part_range = slice(parts[0], parts[-1] + 1)
            nc.scalar.copy(out=turned[t][:, part_range, :], in_=turned_ps[:, part_range, :])

        warm_up(3)
        turn(0, (0,))
        warm_up(1)
        b1_planes = consts.tile([P, PACK, P], BF16)
        nc.vector.tensor_copy(out=b1_planes[:], in_=b1_row[:].rearrange("o (p j) -> o j p", j=PACK))
        b2_ps = vector_bank([P, 2 * LS, P], BF16)
        for l in range(LS):
            nc.tensor.transpose(b2_ps[:, l, :], b2_row[:, l:SECTION:LS], ident_bf[:])
        for part in range(LS):
            nc.tensor.transpose(b2_ps[:, LS + part, :], b2_row[:, part * P : (part + 1) * P], ident_bf[:])
        bias = consts.tile([P, 2 * LS, 4], F32)
        nc.vector.tensor_copy(out=bias[:], in_=b2_ps[:, :, 0:4])
        def hidden_block(t, r):
            if r == 0:
                grouped[t] = hidden.tile([P, COLS, PACK], BF16, name="grouped", align_bytes=64)
            h_ps = scalar_bank([P, PACK, P], F32)
            for j in range(PACK):
                if t < MATMUL_BIAS_ROUNDS:
                    nc.tensor.matmul(out=h_ps[:, j, :], lhsT=b1_planes[:, j, :], rhs=ones[:], start=True, stop=False)
                else:
                    nc.tensor.matmul(
                        out=h_ps[:, j, :], lhsT=b1_rows[:, j, :], rhs=ident_f[:], is_transpose=True, start=True, stop=False
                    )
                nc.tensor.matmul(
                    out=h_ps[:, j, :], lhsT=w1_r[:, j, :], rhs=turned[t][:, 0, r * P : (r + 1) * P],
                    start=False, stop=True,
                )
            nc.scalar.activation(
                out=grouped[t][:, r * P : (r + 1) * P, :], in_=h_ps[:].rearrange("p j w -> p w j"), func=ACT.Relu
            )

        def quantise_hidden(t):
            h_codes[t] = hidden.tile([P, COLS], U32, name="h_codes", align_bytes=64)
            h_scales[t] = hidden.tile([P, COLS], U8, name="h_scales", align_bytes=64)
            nc.vector.quantize_mx(
                out=h_codes[t][:].bitcast(FP8X4),
                scales=h_scales[t][:],
                in_=grouped[t][:].rearrange("p w j -> p (w j)"),
            )

        w2_grp = consts.tile([P, len(CHUNKS), P, PACK], BF16, align_bytes=64)
        w2_codes = consts.tile([P, len(CHUNKS), P], U32, align_bytes=64)
        w2_scales = consts.tile([P, len(CHUNKS), P], U8, align_bytes=64)

        def group_chunk(c):
            s, l = CHUNKS[c]
            nc.vector.tensor_copy(
                out=w2_grp[:, c, :, :], in_=w2_raw[s][:].rearrange("p j (d l) -> p l d j", l=LS)[:, l, :, :]
            )

        def quantise_chunks(first, end):
            nc.vector.quantize_mx(
                out=w2_codes[:, first:end, :].rearrange("p c d -> p (c d)").bitcast(FP8X4),
                scales=w2_scales[:, first:end, :].rearrange("p c d -> p (c d)"),
                in_=w2_grp[:, first:end, :, :].rearrange("p c d j -> p (c d j)"),
            )

        def group_last_section(part):
            nc.gpsimd.tensor_scalar(
                out=w2_grp[:, 9 + part, :, :], in0=w2_raw[3][:].rearrange("p j (s d) -> p s d j", s=LS)[:, part, :, :],
                scalar1=1.0, scalar2=0.0, op0=ALU.mult, op1=ALU.add,
            )

        def params(t, section, part, bank):
            c = CHUNKS.index((section, part))
            p_ps = bank([P, COLS], F32)
            nc.tensor.matmul_mx(
                out=p_ps[:],
                lhsT=w2_codes[:, c, :].bitcast(FP8X4),
                lhsT_scale=w2_scales[:, c, :],
                rhs=h_codes[t][:].bitcast(FP8X4),
                rhs_scale=h_scales[t][:],
                start=True,
                stop=True,
            )
            return p_ps

        def transposed_sum(terms, bank, blocks=range(BLOCKS)):
            total = bank([P, BLOCKS, P], F32)
            for r in blocks:
                for i, term in enumerate(terms):
                    nc.tensor.matmul(
                        out=total[:, r, :],
                        lhsT=term[:, r * P : (r + 1) * P],
                        rhs=ident_f[:],
                        is_transpose=True,
                        start=(i == 0),
                        stop=(i == len(terms) - 1),
                    )
            return total[:].rearrange("p r d -> p (r d)")[:, blocks[0] * P : (blocks[-1] + 1) * P]

        mat2 = {}
        mat1_ps = {}
        bias1_ps = {}
        den_term = {}
        x_mat1 = {}
        z_plus_one = {}
        exp_z = {}
        elu_plus_one = {}
        num_term = {}
        tanh_eps = {}
        exp_alpha = {}
        bias2 = {}
        sigmoid_eps = {}
        gate = {}
        x_scaled = {}
        log_den = {}
        inv_den = {}
        ratio = {}
        moved = {}
        sums = {}

        def mat2_pass(g):
            t, l = divmod(g, LS)
            mat2_ps = params(t, MAT2, l, scalar_bank)
            if g % 2 == 0:
                mat2[g // 2] = work.tile([P, 2, COLS], F32, name="mat2", bufs=4)
            nc.scalar.activation(
                out=mat2[g // 2][:, g % 2, :], in_=mat2_ps[:], func=ACT.Identity, bias=bias[:, l, MAT2 : MAT2 + 1], scale=1.0
            )

        def mat1_pass(g):
            t, l = divmod(g, LS)
            mat1_ps[g] = params(t, MAT1, l, vector_bank)

        def bias1_pass(g):
            t, l = divmod(g, LS)
            bias1_ps[g] = params(t, BIAS1, l, vector_bank)

        def x_product(g):
            t, l = divmod(g, LS)
            if g % 2 == 0:
                z_plus_one[g // 2] = work.tile([P, 2, COLS], F32, name="z_plus_one", bufs=3)
            nc.vector.scalar_tensor_tensor(
                out=z_plus_one[g // 2][:, g % 2, :], in0=mat1_ps[g][:], scalar=bias[:, l, MAT1 : MAT1 + 1],
                in1=turned[t][:, 1, :], op0=ALU.add, op1=ALU.mult,
            )

        def mat_product(g):
            t, l = divmod(g, LS)
            den_term[g] = kept.tile([P, COLS], F32, name="den_term", bufs=12)
            nc.vector.scalar_tensor_tensor(
                out=den_term[g][:], in0=mat1_ps[g][:], scalar=bias[:, l, MAT1 : MAT1 + 1],
                in1=mat2[g // 2][:, g % 2, :], op0=ALU.add, op1=ALU.mult,
            )
            nc.gpsimd.tensor_scalar(
                out=den_term[g][:], in0=den_term[g][:], scalar1=0.0, scalar2=LOWEST, op0=ALU.min, op1=ALU.max
            )

        def z_step(g):
            l = g % LS
            z = z_plus_one[g // 2][:, g % 2, :]
            nc.vector.scalar_tensor_tensor(
                out=z, in0=bias1_ps[g][:], scalar=bias1_plus_one[:, l : l + 1], in1=z, op0=ALU.add, op1=ALU.add,
            )

        def exp_step(pair, part):
            if pair not in exp_z:
                exp_z[pair] = kept.tile([P, 2, COLS], F32, name="num_term", bufs=NT)
                for j in range(2):
                    num_term[2 * pair + j] = exp_z[pair][:, j, :]
            nc.scalar.activation(
                out=exp_z[pair][:, part, :], in_=z_plus_one[pair][:, part, :], func=ACT.Exp, bias=minus_one[:], scale=1.0
            )

        def elu_step(pair, part):
            value = exp_z[pair][:, part, :]
            nc.vector.scalar_tensor_tensor(
                out=value, in0=value, scalar=1.0, in1=z_plus_one[pair][:, part, :], op0=ALU.min, op1=ALU.max,
            )

        def term_step(pair, part):
            value = exp_z[pair][:, part, :]
            nc.vector.scalar_tensor_tensor(
                out=value, in0=value, scalar=-1.0, in1=mat2[pair][:, part, :], op0=ALU.add, op1=ALU.mult,
            )

        def bias2_pass(t):
            ps = params(t, 3, BIAS2, scalar_bank)
            bias2[t] = kept.tile([P, COLS], F32, name="bias2", bufs=5)
            nc.scalar.activation(
                out=bias2[t][:], in_=ps[:], func=ACT.Identity, bias=bias[:, LS + BIAS2, 3:4], scale=1.0
            )

        def eps_pass(t):
            ps = params(t, 3, EPS, scalar_bank)
            tanh_eps[t] = kept.tile([P, COLS], F32, name="gate", bufs=NG)
            nc.scalar.activation(out=tanh_eps[t][:], in_=ps[:], func=ACT.Tanh, bias=eps_bias[:], scale=0.05)

        def alpha_pass(t):
            ps = params(t, 3, ALPHA, scalar_bank)
            exp_alpha[t] = kept.tile([P, COLS], F32, name="x_scaled", bufs=NG)
            nc.scalar.activation(out=exp_alpha[t][:], in_=ps[:], func=ACT.Exp, bias=alpha_bias[:], scale=0.1)

        def sigmoid_step(t):
            sigmoid_eps[t] = tanh_eps[t]
            nc.gpsimd.tensor_scalar(
                out=sigmoid_eps[t][:], in0=tanh_eps[t][:], scalar1=1.0, scalar2=0.4, op0=ALU.add, op1=ALU.mult
            )

        def gate_step(t):
            gate[t] = sigmoid_eps[t]
            nc.gpsimd.tensor_tensor(out=gate[t][:], in0=sigmoid_eps[t][:], in1=exp_alpha[t][:], op=ALU.mult)

        def x_scaled_step(t):
            x_scaled[t] = exp_alpha[t]
            nc.gpsimd.tensor_tensor(out=x_scaled[t][:], in0=exp_alpha[t][:], in1=turned[t][:, 1, :], op=ALU.mult)

        def log_denominator(t):
            den_ps = transposed_sum([den_term[LS * t + l] for l in range(LS)], scalar_bank)
            log_den[t] = last.tile([P, COLS], F32, name="log_den", bufs=3)
            nc.scalar.activation(out=log_den[t][:], in_=den_ps, func=ACT.Ln, bias=plus_one[:], scale=-1.0)

        def inverse_denominator(t):
            inv_den[t] = last.tile([P, COLS], F32, name="inv_den")
            nc.scalar.activation(out=inv_den[t][:], in_=log_den[t][:], func=ACT.Exp, scale=-1.0)

        def finish_sum(step, t, bank):
            terms = (
                [num_term[LS * t + l] for l in range(LS)] if step == 0 else [gate[t]] if step == 1 else [x_scaled[t], bias2[t]]
            )
            sums[step, t] = transposed_sum(terms, bank)

        def finish(step, t):
            if step == 0:
                ratio[t] = last.tile([P, COLS], F32, name="ratio")
                nc.vector.tensor_tensor(out=ratio[t][:], in0=sums[0, t], in1=inv_den[t][:], op=ALU.mult)
            elif step == 1:
                moved[t] = last.tile([P, COLS], F32, name="moved")
                nc.vector.tensor_tensor(out=moved[t][:], in0=sums[1, t], in1=ratio[t][:], op=ALU.mult)
            else:
                result = last.tile([P, BLOCKS, DIM], F32, name="result")
                nc.vector.tensor_tensor(
                    out=result[:].rearrange("p r d -> p (r d)"), in0=sums[2, t], in1=moved[t][:], op=ALU.add
                )
                nc.sync.dma_start(out=out_rows[:, t * BLOCKS : (t + 1) * BLOCKS, :], in_=result[:])

        for r in range(BLOCKS):
            hidden_block(0, r)
        turn(0, (1,))
        group_chunk(0)
        group_chunk(1)
        bias1_plus_one = consts.tile([P, LS], F32)
        nc.vector.tensor_scalar_add(out=bias1_plus_one[:], in0=bias[:, 0:LS, BIAS1], scalar1=1.0)
        eps_bias = consts.tile([P, 1], F32)
        nc.vector.tensor_scalar_mul(out=eps_bias[:], in0=bias[:, LS + EPS, 3:4], scalar1=0.05)
        alpha_bias = consts.tile([P, 1], F32)
        nc.vector.tensor_scalar_mul(out=alpha_bias[:], in0=bias[:, LS + ALPHA, 3:4], scalar1=0.1)
        for c in range(2, 5):
            group_chunk(c)
        quantise_chunks(0, 4)
        turn(1, (0, 1))
        quantise_hidden(0)
        mat1_pass(0)
        mat2_pass(0)
        bias1_pass(0)
        for c in range(5, 9):
            group_chunk(c)
        quantise_chunks(4, 8)
        x_product(0)
        hidden_block(1, 0)
        hidden_block(1, 1)

        turns = {0: 2, 2: 3}
        blocks = {0: [(1, 2), (1, 3)], 1: [(2, 0), (2, 1)], 2: [(2, 2), (2, 3)], 3: [(3, 0), (3, 1)], 4: [(3, 2), (3, 3)]}
        for t in range(4, ROUNDS):
            turns[LS * (t - 2) - 1] = t
            for l in (0, 1):
                blocks[LS * (t - 2) + l] = [(t, 2 * l), (t, 2 * l + 1)]
        quantise_at = {2: 1}
        for t in range(2, ROUNDS):
            quantise_at[LS * (t - 1) + 1] = t

        logs_at = {8: (0, 1, 2), 17: (3, 4, 5)}
        steps = [(step, t) for t in range(ROUNDS) for step in range(LS)]
        finishes = {}
        both = slice(0, 2)
        first = slice(0, 1)
        second = slice(1, 2)
        for g, count in FIN:
            finishes[g] = [steps.pop(0) for i in range(count)]

        passes = [[] for g in range(SLOTS)]
        products = [[] for g in range(SLOTS)]
        for t in range(ROUNDS):
            for l, step in enumerate((bias2_pass, eps_pass, alpha_pass)):
                passes[LS * (t + 1) + l if t < 5 else (18, 18, 19, 19, 20, 20, 21, 21, 21)[LS * (t - 5) + l]].append((step, t))
            for l, step in enumerate((sigmoid_step, gate_step, x_scaled_step)):
                products[LS * (t + 1) + 2 + l if t < 5 else (19, 20, 20, 21, 21, 22, 22, 23, 23)[LS * (t - 5) + l]].append((step, t))
        mat1_early = {0: (1,), 2: (3,)}
        mat1_late = {1: ()}
        for g in range(SLOTS - LS):
            t, l = divmod(g, LS)
            if g in quantise_at:
                quantise_hidden(quantise_at[g])
            mat_product(g)
            z_step(g)
            for ahead in mat1_early.get(g, ()):
                mat1_pass(ahead)
            bias1_pass(g + 1)
            mat2_pass(g + 1)
            if g < 18:
                for step, r in passes[g]:
                    step(r)
            for ahead in mat1_late.get(g, (g + 2,)):
                mat1_pass(ahead)
            if g == SLOTS - LS - 1:
                mat1_pass(g + 3)
                mat2_pass(g + 2)
            if g == 0:
                group_last_section(0)
                group_last_section(1)
            if g == 1:
                group_last_section(2)
            if g == 4:
                nc.gpsimd.tensor_scalar(
                    out=b1_rows[:], in0=b1_all[:].rearrange("w (p j) -> w j p", j=PACK),
                    scalar1=1.0, scalar2=0.0, op0=ALU.mult, op1=ALU.add,
                )
            for step, r in products[g]:
                step(r)
            following = finishes.get(g + 1, ())
            for step, r in following:
                if step == 0:
                    inverse_denominator(r)
            if EXP2:
                if g % 2 == 1:
                    exp_step(g // 2, both)
            else:
                exp_step(g // 2, slice(g % 2, g % 2 + 1))
            if g >= 18:
                for step, r in passes[g]:
                    step(r)
            x_product(g + 1)
            now = finishes.get(g, ())
            if len(now) > 0:
                finish(*now[0])
            if len(now) > 1:
                finish_sum(*now[1], sum_bank)
            if g >= 2:
                if g % 2 == 0:
                    elu_step(g // 2 - 1, both)
                if g % 2 == 1:
                    term_step(g // 2 - 1, both)
            if len(now) > 1:
                finish(*now[1])
            if g == 0:
                quantise_chunks(8, 9)
            if g == 2:
                quantise_chunks(9, 11)
                quantise_chunks(11, 12)
            if g in turns:
                turn(turns[g], (0, 1))
            for block in blocks.get(g, ()):
                hidden_block(*block)
            for r in logs_at.get(g, ()):
                log_denominator(r)
            if g == SLOTS - LS - 1:
                finish_sum(*steps[0], sum_bank)
            if len(following) > 0:
                finish_sum(*following[0], sum_bank)

        n = SLOTS - LS
        t = ROUNDS - 1
        steps[1:7] = [(0, 4), (0, 5), (1, 4), (1, 5), (2, 4), (2, 5)]
        summed = steps[1:]

        def sum_next(bank):
            step = summed.pop(0)
            finish_sum(*step, bank)

        def finish_next():
            step = steps.pop(0)
            finish(*step)

        mat_product(n)
        z_step(n)
        mat2_pass(n + 2)
        bias1_pass(n + 1)
        inverse_denominator(4)
        exp_step(n // 2, both if EXP2 else second)
        for step, r in passes[n]:
            step(r)
        inverse_denominator(5)
        bias1_pass(n + 2)
        for step, r in products[n]:
            step(r)
        x_product(n + 1)
        mat_product(n + 1)
        finish_next()
        sum_next(sum_bank)
        mat_product(n + 2)
        x_product(n + 2)
        for step, r in products[n + 1] + products[n + 2]:
            step(r)
        term_step(n // 2 - 1, both)
        log_denominator(t - 1)
        log_denominator(t)
        sum_next(vector_bank)
        sum_next(vector_bank)
        z_step(n + 1)
        z_step(n + 2)
        sum_next(vector_bank)
        sum_next(vector_bank)
        elu_step(n // 2, both)
        finish_next()
        sum_next(sum_bank)
        term_step(n // 2, both)
        finish_next()
        sum_next(vector_bank)
        finish_next()
        sum_next(vector_bank)
        finish_next()
        sum_next(vector_bank)
        finish_next()
        finish_next()
        exp_step(n // 2 + 1, first)
        exp_step(n // 2 + 1, second)
        inverse_denominator(t - 1)
        inverse_denominator(t)
        elu_step(n // 2 + 1, first)
        elu_step(n // 2 + 1, second)
        finish_next()
        term_step(n // 2 + 1, first)
        finish_next()
        term_step(n // 2 + 1, second)
        finish_sum(1, t, vector_bank)
        finish_sum(2, t, vector_bank)
        halves = (range(0, 2), range(2, BLOCKS))
        last_sums = [transposed_sum([num_term[LS * t + l] for l in range(LS)], bank, half) for bank, half in ((sum_bank, halves[0]), (vector_bank, halves[1]))]
        finish_next()
        ratio[t] = last.tile([P, COLS], F32, name="ratio")
        moved[t] = last.tile([P, COLS], F32, name="moved")
        result = last.tile([P, BLOCKS, DIM], F32, name="result")
        flat = result[:].rearrange("p r d -> p (r d)")
        for half in range(2):
            cols = slice(half * 2 * P, (half + 1) * 2 * P)
            nc.vector.tensor_tensor(out=ratio[t][:, cols], in0=last_sums[half], in1=inv_den[t][:, cols], op=ALU.mult)
        for half in range(2):
            cols = slice(half * 2 * P, (half + 1) * 2 * P)
            nc.vector.tensor_tensor(out=moved[t][:, cols], in0=sums[1, t][:, cols], in1=ratio[t][:, cols], op=ALU.mult)
        for half in range(2):
            cols = slice(half * 2 * P, (half + 1) * 2 * P)
            nc.vector.tensor_tensor(out=flat[:, cols], in0=sums[2, t][:, cols], in1=moved[t][:, cols], op=ALU.add)
            nc.sync.dma_start(
                out=out_rows[:, t * BLOCKS + 2 * half : t * BLOCKS + 2 * half + 2, :],
                in_=result[:, 2 * half : 2 * half + 2, :],
            )
